import numpy as np
import ml_dtypes


def mxq(x, axis, fmt="e4m3"):
    dtype, down = {"e4m3": (ml_dtypes.float8_e4m3fn, 7), "e5m2": (ml_dtypes.float8_e5m2, 14)}[fmt]
    v = np.moveaxis(np.asarray(x, np.float32).astype(ml_dtypes.bfloat16).astype(np.float64), axis, -1)
    blocks = v.reshape(v.shape[:-1] + (-1, 32))
    amax = np.abs(blocks).max(-1, keepdims=True)
    byte = np.maximum(np.where(amax > 0, np.frexp(amax)[1] - 1 + 127, 0) - down, 1)
    scale = np.exp2(byte - 127.0)
    codes = (blocks / scale).astype(np.float32).astype(dtype).astype(np.float64)
    return np.moveaxis((codes * scale).reshape(v.shape), -1, axis)


WIDE = False


def mx_kscale(k):
    if not WIDE:
        return np.ones(k)
    levels = np.array([10, -10, 5, -5, 0])
    a = np.random.permutation(np.resize(levels, k // 512 * 4)).reshape(k // 512, 4)
    idx = np.arange(k)
    return np.exp2(a[idx // 512, idx % 128 // 32])


BF16 = ml_dtypes.bfloat16


def bf(x):
    return np.asarray(x, np.float32).astype(BF16)


def f64(x):
    return np.asarray(x).astype(np.float64)


B, T, D, NH, HD, G, RD, F = 2, 2048, 256, 8, 128, 2, 16, 4096
HKV = NH // G
C = NH * HD


def setup_inputs():
    s = mx_kscale(C).reshape(NH, HD)
    sh = np.where(np.arange(NH) % 2 == 0, s.max(axis=1), s.min(axis=1))
    v = np.random.standard_normal((B, HKV, T, HD))
    a = 0.4 * np.random.standard_normal((B, HKV, G, T, HD)) + 0.4 * v[:, :, None]
    return {"attn_out": bf(a * sh.reshape(HKV, G)[None, :, :, None, None]),
            "v": bf(v),
            "x": bf(np.random.standard_normal((B, T, D)) * np.random.uniform(0.5, 2.0, (B, T, 1))),
            "wo": bf(np.random.standard_normal((D, C)) / np.sqrt(C) / np.repeat(sh, HD)[None, :]),
            "attn_scale": bf(1.0 + 0.1 * np.random.standard_normal(D))}


def reference(attn_out, v, x, wo, attn_scale):
    y_g = f64(attn_out).transpose(0, 3, 1, 2, 4)
    v_t = f64(v).transpose(0, 2, 1, 3)
    vn = v_t / np.maximum(np.sqrt(np.sum(np.square(v_t), axis=-1, keepdims=True)), 1e-12)
    vn = vn[:, :, :, None, :]
    proj = np.sum(y_g * vn, axis=-1, keepdims=True) * vn
    y = (y_g - proj).reshape(B, T, C)
    return f64(x) + f64(attn_scale) * (mxq(y, 2, "e4m3") @ mxq(f64(wo), 1, "e4m3").T)

@@ -1,0 +1,336 @@
+from contextlib import ExitStack
+
+import concourse.mybir as mybir
+from concourse.masks import make_identity
+
+BF16 = mybir.dt.bfloat16
+F32 = mybir.dt.float32
+U32 = mybir.dt.uint32
+U8 = mybir.dt.uint8
+FP8X4 = mybir.dt.float8_e4m3fn_x4
+ALU = mybir.AluOpType
+ACT = mybir.ActivationFunctionType
+
+BATCH, SEQ, CHANNELS = 2, 2048, 256
+KV_HEADS, GROUP, HEAD_DIM = 4, 2, 128
+HEADS = KV_HEADS * GROUP
+K = HEADS * HEAD_DIM
+
+P = 128
+PACK = 4
+K_PASS = P * PACK
+PASSES = K // K_PASS
+PAIR = 2
+WORDS_PASS = K_PASS // PAIR
+HALVES = CHANNELS // P
+
+TILES = 4
+CHUNK = P * TILES
+CHUNKS_PER_BATCH = SEQ // CHUNK
+CHUNKS = BATCH * CHUNKS_PER_BATCH
+ROW = TILES * HEAD_DIM
+BANK = 512
+PART_TILES = BANK // CHANNELS
+PARTS = TILES // PART_TILES
+PART = PART_TILES * P
+
+NORM_FLOOR_SQUARED = 1e-24
+
+FLOPS = 2 * BATCH * SEQ * K * CHANNELS
+
+
+def transpose_words(nc, turned_halves, words, identity):
+    for u in range(PAIR):
+        nc.tensor.transpose(turned_halves[u], words[:, u:WORDS_PASS:PAIR], identity)
+
+
+def tile_block_pb_t_kernel(tc, attn_out, v, x, wo, attn_scale, out):
+    nc = tc.nc
+    with ExitStack() as scope:
+        const = scope.enter_context(tc.tile_pool(name="const", bufs=1))
+        inputs = scope.enter_context(tc.tile_pool(name="inputs", bufs=4))
+        work = scope.enter_context(tc.tile_pool(name="work", bufs=2))
+        parts = scope.enter_context(tc.tile_pool(name="parts", bufs=2 * PARTS))
+        small = scope.enter_context(tc.tile_pool(name="small", bufs=3))
+        turned_banks = scope.enter_context(tc.psum_pool(name="turned_banks", bufs=TILES))
+        sum_banks = scope.enter_context(tc.psum_pool(name="sum_banks", bufs=PARTS))
+        out_banks = scope.enter_context(tc.psum_pool(name="out_banks", bufs=PARTS))
+
+        a_of, v_of, x_of = {}, {}, {}
+        norm2_of, floored_of, inverse_of, dot_of, factor_of = {}, {}, {}, {}, {}
+        turned_of, grouped_of, codes_of, scales_of = {}, {}, {}, {}
+        sums_of, scaled_of, back_of = {}, {}, {}
+
+        identity = const.tile([P, P], F32)
+        make_identity(nc, identity[:])
+
+        wo_rows = const.tile([P, HALVES, K], BF16)
+        nc.scalar.dma_start(out=wo_rows[:], in_=wo.rearrange("(half p) k -> p half k", p=P))
+        gain_rows = const.tile([P, CHANNELS], BF16)
+        nc.scalar.dma_start(out=gain_rows[:], in_=attn_scale.partition_broadcast(P))
+        wo_grouped = const.tile([P, PASSES, CHANNELS, PACK], BF16, align_bytes=64)
+        wo_codes = const.tile([P, PASSES, CHANNELS], U32, align_bytes=64)
+        wo_scales = const.tile([P, PASSES, CHANNELS], U8, align_bytes=64)
+        gain_column = const.tile([P, HALVES], F32)
+
+        def prepare_wo_and_gain():
+            wo_words = wo_rows[:].bitcast(F32)
+            grouped_words = wo_grouped[:].bitcast(F32)
+            for c in range(PASSES):
+                turned = turned_banks.tile([P, PAIR, CHANNELS], F32, tag="turned")
+                for half in range(HALVES):
+                    transpose_words(
+                        nc,
+                        [turned[:, u, half * P : (half + 1) * P] for u in range(PAIR)],
+                        wo_words[:, half, c * WORDS_PASS : (c + 1) * WORDS_PASS],
+                        identity[:],
+                    )
+                nc.scalar.copy(out=grouped_words[:, c], in_=turned[:].rearrange("p u n -> p n u"))
+            nc.vector.quantize_mx(
+                out=wo_codes[:].rearrange("p c n -> p (c n)").bitcast(FP8X4),
+                scales=wo_scales[:].rearrange("p c n -> p (c n)"),
+                in_=wo_grouped[:].rearrange("p c n k -> p (c n k)"),
+            )
+            gain_wide = const.tile([P, CHANNELS], F32)
+            nc.scalar.copy(out=gain_wide[:], in_=gain_rows[:])
+            turned = turned_banks.tile([P, HALVES, P], F32, tag="turned")
+            for half in range(HALVES):
+                nc.tensor.transpose(
+                    turned[:, half, :], gain_wide[:, half * P : (half + 1) * P], identity[:]
+                )
+            nc.scalar.copy(out=gain_column[:], in_=turned[:, :, 0])
+
+        def tokens_of(chunk):
+            b, n = divmod(chunk, CHUNKS_PER_BATCH)
+            return b, slice(n * CHUNK, (n + 1) * CHUNK)
+
+        def load(chunk):
+            b, tokens = tokens_of(chunk)
+            v_rows = inputs.tile([P, KV_HEADS, ROW], BF16)
+            a_rows = inputs.tile([P, HEADS, ROW], BF16)
+            for h in range(KV_HEADS):
+                nc.sync.dma_start(
+                    out=v_rows[:, h, :],
+                    in_=v[b, h, tokens, :].rearrange("(p i) d -> p (i d)", i=TILES),
+                )
+                nc.sync.dma_start(
+                    out=a_rows[:, h * GROUP : (h + 1) * GROUP, :],
+                    in_=attn_out[b, h, :, tokens, :].rearrange("g (p i) d -> p g (i d)", i=TILES),
+                )
+            a_of[chunk], v_of[chunk] = a_rows, v_rows
+
+        def load_residual(chunk):
+            b, tokens = tokens_of(chunk)
+            x_rows = inputs.tile([P, TILES * CHANNELS], BF16)
+            nc.sync.dma_start(
+                out=x_rows[:], in_=x[b, tokens, :].rearrange("(p i) n -> p (i n)", i=TILES)
+            )
+            x_of[chunk] = x_rows
+
+        def squared_norms(chunk):
+            v_rows = v_of[chunk]
+            norm2 = small.tile([P, KV_HEADS * TILES], F32)
+            squares_unread = work.tile([P, KV_HEADS, ROW], BF16)
+            for h in range(KV_HEADS):
+                for i in range(TILES):
+                    dims = slice(i * HEAD_DIM, (i + 1) * HEAD_DIM)
+                    nc.scalar.activation(
+                        out=squares_unread[:, h, dims],
+                        in_=v_rows[:, h, dims],
+                        func=ACT.Square,
+                        accum_out=norm2[:, h * TILES + i : h * TILES + i + 1],
+                    )
+            norm2_of[chunk] = norm2
+
+        def dot_products(chunk):
+            a_rows, v_rows = a_of[chunk], v_of[chunk]
+            products = work.tile([P, HEADS, ROW], F32)
+            for h in range(KV_HEADS):
+                heads = slice(h * GROUP, (h + 1) * GROUP)
+                nc.vector.tensor_tensor(
+                    out=products[:, heads, :],
+                    in0=a_rows[:, heads, :],
+                    in1=v_rows[:, h : h + 1, :].to_broadcast([P, GROUP, ROW]),
+                    op=ALU.mult,
+                )
+            dot = small.tile([P, HEADS * TILES], F32)
+            products_unread = work.tile([P, HEADS, ROW], BF16)
+            for head in range(HEADS):
+                for i in range(TILES):
+                    dims = slice(i * HEAD_DIM, (i + 1) * HEAD_DIM)
+                    nc.scalar.activation(
+                        out=products_unread[:, head, dims],
+                        in_=products[:, head, dims],
+                        func=ACT.Copy,
+                        accum_out=dot[:, head * TILES + i : head * TILES + i + 1],
+                    )
+            dot_of[chunk] = dot
+
+        def floor_norms(chunk):
+            floored = small.tile([P, KV_HEADS, TILES], F32)
+            nc.vector.tensor_scalar(
+                out=floored[:].rearrange("p h i -> p (h i)"),
+                in0=norm2_of[chunk][:],
+                scalar1=-1.0,
+                scalar2=-NORM_FLOOR_SQUARED,
+                op0=ALU.mult,
+                op1=ALU.min,
+            )
+            floored_of[chunk] = floored
+
+        def invert_norms(chunk):
+            inverse = small.tile([P, KV_HEADS, TILES], F32)
+            nc.vector.reciprocal(out=inverse[:], in_=floored_of[chunk][:])
+            inverse_of[chunk] = inverse
+
+        def factors(chunk):
+            factor = small.tile([P, HEADS * TILES], F32)
+            nc.vector.tensor_tensor(
+                out=factor[:].rearrange("p (h g i) -> p h g i", g=GROUP, i=TILES),
+                in0=dot_of[chunk][:].rearrange("p (h g i) -> p h g i", g=GROUP, i=TILES),
+                in1=inverse_of[chunk][:].unsqueeze(2).to_broadcast([P, KV_HEADS, GROUP, TILES]),
+                op=ALU.mult,
+            )
+            factor_of[chunk] = factor
+
+        def project_and_transpose(chunk):
+            a_rows, v_rows, factor = a_of[chunk], v_of[chunk], factor_of[chunk]
+            y = work.tile([P, TILES, K], BF16)
+            y_words = y[:].bitcast(F32)
+            turned_of[chunk] = []
+            for i in range(TILES):
+                dims = slice(i * HEAD_DIM, (i + 1) * HEAD_DIM)
+                for head in range(HEADS):
+                    nc.vector.scalar_tensor_tensor(
+                        out=y[:, i, head * HEAD_DIM : (head + 1) * HEAD_DIM],
+                        in0=v_rows[:, head // GROUP, dims],
+                        scalar=factor[:, head * TILES + i : head * TILES + i + 1],
+                        in1=a_rows[:, head, dims],
+                        op0=ALU.mult,
+                        op1=ALU.add,
+                    )
+                turned = turned_banks.tile([P, PASSES, PAIR, P], F32, tag="turned")
+                for c in range(PASSES):
+                    transpose_words(
+                        nc,
+                        [turned[:, c, u, :] for u in range(PAIR)],
+                        y_words[:, i, c * WORDS_PASS : (c + 1) * WORDS_PASS],
+                        identity[:],
+                    )
+                turned_of[chunk].append(turned)
+
+        def regroup(chunk, part):
+            grouped = parts.tile([P, PASSES, PART_TILES, P, PACK], BF16, align_bytes=64)
+            grouped_words = grouped[:].bitcast(F32)
+            for j in range(PART_TILES):
+                nc.scalar.copy(
+                    out=grouped_words[:, :, j],
+                    in_=turned_of[chunk][part * PART_TILES + j][:].rearrange("p c u t -> p c t u"),
+                )
+            grouped_of[chunk, part] = grouped
+
+        def quantise(chunk, part):
+            codes = parts.tile([P, PASSES, PART], U32, align_bytes=64)
+            scales = parts.tile([P, PASSES, PART], U8, align_bytes=64)
+            nc.vector.quantize_mx(
+                out=codes[:].rearrange("p c t -> p (c t)").bitcast(FP8X4),
+                scales=scales[:].rearrange("p c t -> p (c t)"),
+                in_=grouped_of[chunk, part][:].rearrange("p c j t k -> p (c j t k)"),
+            )
+            codes_of[chunk, part], scales_of[chunk, part] = codes, scales
+
+        def multiply(chunk, part):
+            codes, scales = codes_of[chunk, part], scales_of[chunk, part]
+            sums = sum_banks.tile([P, HALVES, PART], F32)
+            for half in range(HALVES):
+                channels = slice(half * P, (half + 1) * P)
+                for c in range(PASSES):
+                    nc.tensor.matmul_mx(
+                        out=sums[:, half, :],
+                        lhsT=wo_codes[:, c, channels].bitcast(FP8X4),
+                        lhsT_scale=wo_scales[:, c, channels],
+                        rhs=codes[:, c, :].bitcast(FP8X4),
+                        rhs_scale=scales[:, c, :],
+                        start=(c == 0),
+                        stop=(c == PASSES - 1),
+                    )
+            sums_of[chunk, part] = sums
+
+        def apply_gain(chunk, part):
+            scaled = parts.tile([P, HALVES, PART], F32)
+            for half in range(HALVES):
+                nc.scalar.activation(
+                    out=scaled[:, half, :],
+                    in_=sums_of[chunk, part][:, half, :],
+                    func=ACT.Copy,
+                    scale=gain_column[:, half : half + 1],
+                )
+            scaled_of[chunk, part] = scaled
+
+        def transpose_back(chunk, part):
+            scaled = scaled_of[chunk, part]
+            back = out_banks.tile([P, PART_TILES, CHANNELS], F32)
+            for j in range(PART_TILES):
+                for half in range(HALVES):
+                    nc.tensor.transpose(
+                        back[:, j, half * P : (half + 1) * P],
+                        scaled[:, half, j * P : (j + 1) * P],
+                        identity[:],
+                    )
+            back_of[chunk, part] = back
+
+        def add_residual_and_store(chunk, part):
+            b, tokens = tokens_of(chunk)
+            result = parts.tile([P, PART_TILES, CHANNELS], F32)
+            nc.vector.tensor_tensor(
+                out=result[:].rearrange("p j n -> p (j n)"),
+                in0=back_of[chunk, part][:].rearrange("p j n -> p (j n)"),
+                in1=x_of[chunk][:, part * BANK : (part + 1) * BANK],
+                op=ALU.add,
+            )
+            queue = nc.sync if chunk == CHUNKS - 1 else nc.gpsimd
+            tiles = slice(part * PART_TILES, (part + 1) * PART_TILES)
+            queue.dma_start(
+                out=out[b, tokens, :].rearrange("(p i) n -> p i n", i=TILES)[:, tiles, :],
+                in_=result[:],
+            )
+
+        def exists(chunk):
+            return 0 <= chunk < CHUNKS
+
+        load(0)
+        for step in range(CHUNKS + 3):
+            ahead, now, behind, last = step, step - 1, step - 2, step - 3
+            if exists(ahead + 1):
+                load(ahead + 1)
+            if exists(now):
+                load_residual(now)
+            if exists(behind):
+                for part in range(PARTS):
+                    regroup(behind, part)
+            if exists(ahead):
+                squared_norms(ahead)
+                dot_products(ahead)
+            if exists(last):
+                for part in range(PARTS):
+                    add_residual_and_store(last, part)
+            if step == 1:
+                prepare_wo_and_gain()
+            if exists(now):
+                factors(now)
+            if exists(ahead):
+                floor_norms(ahead)
+            if exists(behind):
+                for part in range(PARTS):
+                    quantise(behind, part)
+                    multiply(behind, part)
+            if exists(ahead):
+                invert_norms(ahead)
+            if exists(behind):
+                for part in range(PARTS):
+                    apply_gain(behind, part)
+            if exists(now):
+                project_and_transpose(now)
+            if exists(behind):
+                for part in range(PARTS):
+                    transpose_back(behind, part)

@@ -33,6 +33,9 @@ BANK = 512
 PART_TILES = BANK // CHANNELS
 PARTS = TILES // PART_TILES
 PART = PART_TILES * P
+UNITS = HEADS * TILES
+STEP = UNITS * HEAD_DIM // P
+PHASES = HEAD_DIM // STEP
 
 NORM_FLOOR_SQUARED = 1e-24
 
@@ -52,7 +55,8 @@ def tile_block_pb_t_kernel(tc, attn_out, v, x, wo, attn_scale, out):
         work = scope.enter_context(tc.tile_pool(name="work", bufs=2))
         parts = scope.enter_context(tc.tile_pool(name="parts", bufs=2 * PARTS))
         small = scope.enter_context(tc.tile_pool(name="small", bufs=3))
-        turned_banks = scope.enter_context(tc.psum_pool(name="turned_banks", bufs=TILES))
+        turned_banks = scope.enter_context(tc.psum_pool(name="turned_banks", bufs=TILES - 1))
+        dot_banks = scope.enter_context(tc.psum_pool(name="dot_banks", bufs=1))
         sum_banks = scope.enter_context(tc.psum_pool(name="sum_banks", bufs=PARTS))
         out_banks = scope.enter_context(tc.psum_pool(name="out_banks", bufs=PARTS))
 
@@ -61,6 +65,7 @@ def tile_block_pb_t_kernel(tc, attn_out, v, x, wo, attn_scale, out):
         turned_of, grouped_of, codes_of, scales_of = {}, {}, {}, {}
         sums_of, scaled_of, back_of = {}, {}, {}
 
+        products_of, dot_bank_of = {}, {}
         identity = const.tile([P, P], F32)
         make_identity(nc, identity[:])
 
@@ -142,7 +147,7 @@ def tile_block_pb_t_kernel(tc, attn_out, v, x, wo, attn_scale, out):
                     )
             norm2_of[chunk] = norm2
 
-        def dot_products(chunk):
+        def multiply_elements(chunk):
             a_rows, v_rows = a_of[chunk], v_of[chunk]
             products = work.tile([P, HEADS, ROW], F32)
             for h in range(KV_HEADS):
@@ -153,17 +158,32 @@ def tile_block_pb_t_kernel(tc, attn_out, v, x, wo, attn_scale, out):
                     in1=v_rows[:, h : h + 1, :].to_broadcast([P, GROUP, ROW]),
                     op=ALU.mult,
                 )
+            products_of[chunk] = products
+
+        def sum_products(chunk):
+            flat = products_of[chunk][:].rearrange("p h r -> p (h r)")
+            bank = dot_banks.tile([P, 2, P], F32)
+            for j in range(STEP):
+                nc.tensor.matmul(
+                    out=bank[:, 0, :],
+                    lhsT=flat[:, j::STEP],
+                    rhs=identity[:],
+                    is_transpose=True,
+                    start=(j == 0),
+                    stop=(j == STEP - 1),
+                )
+            phase_sums = small.tile([P, P], F32)
+            nc.scalar.copy(out=phase_sums[:], in_=bank[:, 0, :])
+            nc.tensor.transpose(bank[:, 1, :], phase_sums[:], identity[:])
+            dot_bank_of[chunk] = bank
+
+        def dot_products(chunk):
             dot = small.tile([P, HEADS * TILES], F32)
-            products_unread = work.tile([P, HEADS, ROW], BF16)
-            for head in range(HEADS):
-                for i in range(TILES):
-                    dims = slice(i * HEAD_DIM, (i + 1) * HEAD_DIM)
-                    nc.scalar.activation(
-                        out=products_unread[:, head, dims],
-                        in_=products[:, head, dims],
-                        func=ACT.Copy,
-                        accum_out=dot[:, head * TILES + i : head * TILES + i + 1],
-                    )
+            nc.vector.reduce_sum(
+                out=dot[:],
+                in_=dot_bank_of[chunk][:, 1, :].rearrange("p (u f) -> p u f", f=PHASES),
+                axis=mybir.AxisListType.X,
+            )
             dot_of[chunk] = dot
 
         def floor_norms(chunk):
@@ -310,7 +330,10 @@ def tile_block_pb_t_kernel(tc, attn_out, v, x, wo, attn_scale, out):
                     regroup(behind, part)
             if exists(ahead):
                 squared_norms(ahead)
-                dot_products(ahead)
+                multiply_elements(ahead)
+                sum_products(ahead)
+            if exists(now):
+                dot_products(now)
             if exists(last):
                 for part in range(PARTS):
                     add_residual_and_store(last, part)

@@ -68,6 +68,8 @@ def tile_block_pb_t_kernel(tc, attn_out, v, x, wo, attn_scale, out):
         products_of, dot_bank_of = {}, {}
         identity = const.tile([P, P], F32)
         make_identity(nc, identity[:])
+        identity_bf16 = const.tile([P, P], BF16)
+        nc.scalar.copy(out=identity_bf16[:], in_=identity[:])
 
         wo_rows = const.tile([P, HALVES, K], BF16)
         nc.scalar.dma_start(out=wo_rows[:], in_=wo.rearrange("(half p) k -> p half k", p=P))
@@ -287,27 +289,45 @@ def tile_block_pb_t_kernel(tc, attn_out, v, x, wo, attn_scale, out):
                 )
             scaled_of[chunk, part] = scaled
 
+        def adds_on_tensor(chunk, part):
+            return (chunk * PARTS + part) % 4 != 3
+
         def transpose_back(chunk, part):
             scaled = scaled_of[chunk, part]
             back = out_banks.tile([P, PART_TILES, CHANNELS], F32)
             for j in range(PART_TILES):
                 for half in range(HALVES):
-                    nc.tensor.transpose(
-                        back[:, j, half * P : (half + 1) * P],
-                        scaled[:, half, j * P : (j + 1) * P],
-                        identity[:],
+                    nc.tensor.matmul(
+                        out=back[:, j, half * P : (half + 1) * P],
+                        lhsT=scaled[:, half, j * P : (j + 1) * P],
+                        rhs=identity[:],
+                        is_transpose=True,
+                        start=(half == 0),
+                        stop=(half == HALVES - 1 and not adds_on_tensor(chunk, part)),
+                    )
+                if adds_on_tensor(chunk, part):
+                    i = part * PART_TILES + j
+                    nc.tensor.matmul(
+                        out=back[:, j, :],
+                        lhsT=identity_bf16[:],
+                        rhs=x_of[chunk][:, i * CHANNELS : (i + 1) * CHANNELS],
+                        start=False,
+                        stop=True,
                     )
             back_of[chunk, part] = back
 
         def add_residual_and_store(chunk, part):
             b, tokens = tokens_of(chunk)
             result = parts.tile([P, PART_TILES, CHANNELS], F32)
-            nc.vector.tensor_tensor(
-                out=result[:].rearrange("p j n -> p (j n)"),
-                in0=back_of[chunk, part][:].rearrange("p j n -> p (j n)"),
-                in1=x_of[chunk][:, part * BANK : (part + 1) * BANK],
-                op=ALU.add,
-            )
+            if adds_on_tensor(chunk, part):
+                nc.scalar.copy(out=result[:], in_=back_of[chunk, part][:])
+            else:
+                nc.vector.tensor_tensor(
+                    out=result[:].rearrange("p j n -> p (j n)"),
+                    in0=back_of[chunk, part][:].rearrange("p j n -> p (j n)"),
+                    in1=x_of[chunk][:, part * BANK : (part + 1) * BANK],
+                    op=ALU.add,
+                )
             queue = nc.sync if chunk == CHUNKS - 1 else nc.gpsimd
             tiles = slice(part * PART_TILES, (part + 1) * PART_TILES)
             queue.dma_start(

@@ -25,17 +25,11 @@ WORDS_PASS = K_PASS // PAIR
 HALVES = CHANNELS // P
 
 TILES = 4
-CHUNK = P * TILES
-CHUNKS_PER_BATCH = SEQ // CHUNK
-CHUNKS = BATCH * CHUNKS_PER_BATCH
-ROW = TILES * HEAD_DIM
-BANK = 512
-PART_TILES = BANK // CHANNELS
-PARTS = TILES // PART_TILES
-PART = PART_TILES * P
-UNITS = HEADS * TILES
-STEP = UNITS * HEAD_DIM // P
-PHASES = HEAD_DIM // STEP
+CHUNKS = BATCH * SEQ // (TILES * P)
+WIDE_TILE = 0
+WIDE_PASS = 0
+PASS_HEADS = HEADS // PASSES
+TENSOR_RESIDUAL_CHUNKS = 6
 
 NORM_FLOOR_SQUARED = 1e-24
 
@@ -51,70 +45,40 @@ def tile_block_pb_t_kernel(tc, attn_out, v, x, wo, attn_scale, out):
     nc = tc.nc
     with ExitStack() as scope:
         const = scope.enter_context(tc.tile_pool(name="const", bufs=1))
-        inputs = scope.enter_context(tc.tile_pool(name="inputs", bufs=4))
+        inputs = scope.enter_context(tc.tile_pool(name="inputs", bufs=6))
         work = scope.enter_context(tc.tile_pool(name="work", bufs=2))
-        parts = scope.enter_context(tc.tile_pool(name="parts", bufs=2 * PARTS))
+        parts = scope.enter_context(tc.tile_pool(name="parts", bufs=4))
         small = scope.enter_context(tc.tile_pool(name="small", bufs=3))
-        turned_banks = scope.enter_context(tc.psum_pool(name="turned_banks", bufs=TILES - 1))
-        dot_banks = scope.enter_context(tc.psum_pool(name="dot_banks", bufs=1))
-        sum_banks = scope.enter_context(tc.psum_pool(name="sum_banks", bufs=PARTS))
-        out_banks = scope.enter_context(tc.psum_pool(name="out_banks", bufs=PARTS))
+        turned_banks = scope.enter_context(tc.psum_pool(name="turned_banks", bufs=3))
+        dot_banks = scope.enter_context(tc.psum_pool(name="dot_banks", bufs=2))
+        sum_banks = scope.enter_context(tc.psum_pool(name="sum_banks", bufs=1))
+        out_banks = scope.enter_context(tc.psum_pool(name="out_banks", bufs=2))
+        scope.enter_context(tc.manual_schedule())
 
         a_of, v_of, x_of = {}, {}, {}
         norm2_of, floored_of, inverse_of, dot_of, factor_of = {}, {}, {}, {}, {}
-        turned_of, grouped_of, codes_of, scales_of = {}, {}, {}, {}
+        products_of, dot_bank_of = {}, {}
+        wide_a_of, wide_w_of, y_of = {}, {}, {}
+        turned_of, wide_banks_of, grouped_of, codes_of, scales_of = {}, {}, {}, {}, {}
         sums_of, scaled_of, back_of = {}, {}, {}
 
-        products_of, dot_bank_of = {}, {}
-        identity = const.tile([P, P], F32)
-        make_identity(nc, identity[:])
-        identity_bf16 = const.tile([P, P], BF16)
-        nc.scalar.copy(out=identity_bf16[:], in_=identity[:])
-
-        wo_rows = const.tile([P, HALVES, K], BF16)
-        nc.scalar.dma_start(out=wo_rows[:], in_=wo.rearrange("(half p) k -> p half k", p=P))
-        gain_rows = const.tile([P, CHANNELS], BF16)
-        nc.scalar.dma_start(out=gain_rows[:], in_=attn_scale.partition_broadcast(P))
-        wo_grouped = const.tile([P, PASSES, CHANNELS, PACK], BF16, align_bytes=64)
-        wo_codes = const.tile([P, PASSES, CHANNELS], U32, align_bytes=64)
-        wo_scales = const.tile([P, PASSES, CHANNELS], U8, align_bytes=64)
-        gain_column = const.tile([P, HALVES], F32)
-
-        def prepare_wo_and_gain():
-            wo_words = wo_rows[:].bitcast(F32)
-            grouped_words = wo_grouped[:].bitcast(F32)
-            for c in range(PASSES):
-                turned = turned_banks.tile([P, PAIR, CHANNELS], F32, tag="turned")
-                for half in range(HALVES):
-                    transpose_words(
-                        nc,
-                        [turned[:, u, half * P : (half + 1) * P] for u in range(PAIR)],
-                        wo_words[:, half, c * WORDS_PASS : (c + 1) * WORDS_PASS],
-                        identity[:],
-                    )
-                nc.scalar.copy(out=grouped_words[:, c], in_=turned[:].rearrange("p u n -> p n u"))
-            nc.vector.quantize_mx(
-                out=wo_codes[:].rearrange("p c n -> p (c n)").bitcast(FP8X4),
-                scales=wo_scales[:].rearrange("p c n -> p (c n)"),
-                in_=wo_grouped[:].rearrange("p c n k -> p (c n k)"),
-            )
-            gain_wide = const.tile([P, CHANNELS], F32)
-            nc.scalar.copy(out=gain_wide[:], in_=gain_rows[:])
-            turned = turned_banks.tile([P, HALVES, P], F32, tag="turned")
-            for half in range(HALVES):
-                nc.tensor.transpose(
-                    turned[:, half, :], gain_wide[:, half * P : (half + 1) * P], identity[:]
-                )
-            nc.scalar.copy(out=gain_column[:], in_=turned[:, :, 0])
-
         def tokens_of(chunk):
-            b, n = divmod(chunk, CHUNKS_PER_BATCH)
-            return b, slice(n * CHUNK, (n + 1) * CHUNK)
+            b, first = divmod(chunk * TILES * P, SEQ)
+            return b, slice(first, first + TILES * P)
+
+        def parts_of(chunk):
+            return [[0, 1], [2], [3]] if chunk == CHUNKS - 1 else [[0, 1], [2, 3]]
+
+        def part_of(chunk, i):
+            return [i in tiles for tiles in parts_of(chunk)].index(True)
+
+        def adds_on_tensor(chunk):
+            return chunk < TENSOR_RESIDUAL_CHUNKS
 
         def load(chunk):
             b, tokens = tokens_of(chunk)
-            v_rows = inputs.tile([P, KV_HEADS, ROW], BF16)
-            a_rows = inputs.tile([P, HEADS, ROW], BF16)
+            v_rows = inputs.tile([P, KV_HEADS, TILES * HEAD_DIM], BF16)
+            a_rows = inputs.tile([P, HEADS, TILES * HEAD_DIM], BF16)
             for h in range(KV_HEADS):
                 nc.sync.dma_start(
                     out=v_rows[:, h, :],
@@ -134,65 +98,122 @@ def tile_block_pb_t_kernel(tc, attn_out, v, x, wo, attn_scale, out):
             )
             x_of[chunk] = x_rows
 
-        def squared_norms(chunk):
-            v_rows = v_of[chunk]
-            norm2 = small.tile([P, KV_HEADS * TILES], F32)
-            squares_unread = work.tile([P, KV_HEADS, ROW], BF16)
-            for h in range(KV_HEADS):
+        load(0)
+        load(1)
+        wo_rows = const.tile([P, HALVES, K], BF16)
+        nc.sync.dma_start(out=wo_rows[:], in_=wo.rearrange("(half p) k -> p half k", p=P))
+        gain_rows = const.tile([P, CHANNELS], BF16)
+        nc.gpsimd.memset(gain_rows[:], 0.0)
+        nc.sync.dma_start(out=gain_rows[0:1, :], in_=attn_scale.rearrange("(o n) -> o n", o=1))
+
+        identity = const.tile([P, P], F32)
+        make_identity(nc, identity[:])
+        identity_bf16 = const.tile([P, P], BF16)
+
+        wo_grouped = const.tile([P, PASSES, CHANNELS, PACK], BF16, align_bytes=64)
+        wo_codes = const.tile([P, PASSES, CHANNELS], U32, align_bytes=64)
+        wo_scales = const.tile([P, PASSES, CHANNELS], U8, align_bytes=64)
+        gain_column = const.tile([P, HALVES], F32)
+
+        def turn_wo_and_gain():
+            wo_words = wo_rows[:].bitcast(F32)
+            grouped_words = wo_grouped[:].bitcast(F32)
+            nc.scalar.copy(out=identity_bf16[:], in_=identity[:])
+            for c in range(PASSES):
+                turned = turned_banks.tile([P, PAIR, CHANNELS], F32, tag="turned")
+                for half in range(HALVES):
+                    transpose_words(
+                        nc,
+                        [turned[:, u, half * P : (half + 1) * P] for u in range(PAIR)],
+                        wo_words[:, half, c * WORDS_PASS : (c + 1) * WORDS_PASS],
+                        identity[:],
+                    )
+                nc.scalar.copy(out=grouped_words[:, c], in_=turned[:].rearrange("p u n -> p n u"))
+            gain_wide = const.tile([P, CHANNELS], F32)
+            nc.scalar.copy(out=gain_wide[:], in_=gain_rows[:])
+            turned = turned_banks.tile([P, HALVES, P], F32, tag="turned")
+            for half in range(HALVES):
+                nc.tensor.transpose(
+                    turned[:, half, :], gain_wide[:, half * P : (half + 1) * P], identity[:]
+                )
+            nc.scalar.copy(out=gain_column[:], in_=turned[:, :, 0])
+
+        def quantise_wo():
+            nc.vector.quantize_mx(
+                out=wo_codes[:].rearrange("p c n -> p (c n)").bitcast(FP8X4),
+                scales=wo_scales[:].rearrange("p c n -> p (c n)"),
+                in_=wo_grouped[:].rearrange("p c n k -> p (c n k)"),
+            )
+
+        def squared_norms(chunk, kv_heads):
+            if chunk not in norm2_of:
+                norm2 = small.tile([P, KV_HEADS * TILES], F32)
+                squares_unread = work.tile([P, KV_HEADS, TILES * HEAD_DIM], BF16)
+                norm2_of[chunk] = (norm2, squares_unread)
+            norm2, squares_unread = norm2_of[chunk]
+            for h in kv_heads:
                 for i in range(TILES):
                     dims = slice(i * HEAD_DIM, (i + 1) * HEAD_DIM)
                     nc.scalar.activation(
                         out=squares_unread[:, h, dims],
-                        in_=v_rows[:, h, dims],
+                        in_=v_of[chunk][:, h, dims],
                         func=ACT.Square,
                         accum_out=norm2[:, h * TILES + i : h * TILES + i + 1],
                     )
-            norm2_of[chunk] = norm2
 
-        def multiply_elements(chunk):
-            a_rows, v_rows = a_of[chunk], v_of[chunk]
-            products = work.tile([P, HEADS, ROW], F32)
-            for h in range(KV_HEADS):
-                heads = slice(h * GROUP, (h + 1) * GROUP)
-                nc.vector.tensor_tensor(
-                    out=products[:, heads, :],
-                    in0=a_rows[:, heads, :],
-                    in1=v_rows[:, h : h + 1, :].to_broadcast([P, GROUP, ROW]),
-                    op=ALU.mult,
-                )
-            products_of[chunk] = products
+        def multiply_elements(chunk, h):
+            if chunk not in products_of:
+                products = inputs.tile([P, HEADS, TILES * HEAD_DIM], F32, bufs=3)
+                products_of[chunk] = products
+            heads = slice(h * GROUP, (h + 1) * GROUP)
+            nc.vector.tensor_tensor(
+                out=products_of[chunk][:, heads, :],
+                in0=a_of[chunk][:, heads, :],
+                in1=v_of[chunk][:, h : h + 1, :].to_broadcast([P, GROUP, TILES * HEAD_DIM]),
+                op=ALU.mult,
+            )
 
-        def sum_products(chunk):
+        def sum_products(chunk, quarter):
+            step = HEADS * TILES
             flat = products_of[chunk][:].rearrange("p h r -> p (h r)")
-            bank = dot_banks.tile([P, 2, P], F32)
-            for j in range(STEP):
+            if quarter == 0:
+                dot_bank = dot_banks.tile([P, 2, P], F32)
+                dot_bank_of[chunk] = dot_bank
+            for j in range(quarter * step // 4, (quarter + 1) * step // 4):
                 nc.tensor.matmul(
-                    out=bank[:, 0, :],
-                    lhsT=flat[:, j::STEP],
+                    out=dot_bank_of[chunk][:, 0, :],
+                    lhsT=flat[:, j::step],
                     rhs=identity[:],
                     is_transpose=True,
                     start=(j == 0),
-                    stop=(j == STEP - 1),
+                    stop=(j == step - 1),
                 )
+
+        phase_sums_of = {}
+
+        def copy_phase_sums(chunk):
             phase_sums = small.tile([P, P], F32)
-            nc.scalar.copy(out=phase_sums[:], in_=bank[:, 0, :])
-            nc.tensor.transpose(bank[:, 1, :], phase_sums[:], identity[:])
-            dot_bank_of[chunk] = bank
+            nc.scalar.copy(out=phase_sums[:], in_=dot_bank_of[chunk][:, 0, :])
+            phase_sums_of[chunk] = phase_sums
+
+        def turn_phase_sums(chunk):
+            nc.tensor.transpose(dot_bank_of[chunk][:, 1, :], phase_sums_of[chunk][:], identity[:])
 
         def dot_products(chunk):
-            dot = small.tile([P, HEADS * TILES], F32)
+            units = HEADS * TILES
+            dot = small.tile([P, units], F32)
             nc.vector.reduce_sum(
                 out=dot[:],
-                in_=dot_bank_of[chunk][:, 1, :].rearrange("p (u f) -> p u f", f=PHASES),
+                in_=dot_bank_of[chunk][:, 1, :].rearrange("p (u f) -> p u f", f=P // units),
                 axis=mybir.AxisListType.X,
             )
             dot_of[chunk] = dot
 
         def floor_norms(chunk):
-            floored = small.tile([P, KV_HEADS, TILES], F32)
+            floored = small.tile([P, KV_HEADS * TILES], F32)
             nc.vector.tensor_scalar(
-                out=floored[:].rearrange("p h i -> p (h i)"),
-                in0=norm2_of[chunk][:],
+                out=floored[:],
+                in0=norm2_of[chunk][0][:],
                 scalar1=-1.0,
                 scalar2=-NORM_FLOOR_SQUARED,
                 op0=ALU.mult,
@@ -202,7 +223,9 @@ def tile_block_pb_t_kernel(tc, attn_out, v, x, wo, attn_scale, out):
 
         def invert_norms(chunk):
             inverse = small.tile([P, KV_HEADS, TILES], F32)
-            nc.vector.reciprocal(out=inverse[:], in_=floored_of[chunk][:])
+            nc.vector.reciprocal(
+                out=inverse[:].rearrange("p h i -> p (h i)"), in_=floored_of[chunk][:]
+            )
             inverse_of[chunk] = inverse
 
         def factors(chunk):
@@ -215,45 +238,104 @@ def tile_block_pb_t_kernel(tc, attn_out, v, x, wo, attn_scale, out):
             )
             factor_of[chunk] = factor
 
-        def project_and_transpose(chunk):
-            a_rows, v_rows, factor = a_of[chunk], v_of[chunk], factor_of[chunk]
-            y = work.tile([P, TILES, K], BF16)
-            y_words = y[:].bitcast(F32)
-            turned_of[chunk] = []
-            for i in range(TILES):
-                dims = slice(i * HEAD_DIM, (i + 1) * HEAD_DIM)
-                for head in range(HEADS):
-                    nc.vector.scalar_tensor_tensor(
-                        out=y[:, i, head * HEAD_DIM : (head + 1) * HEAD_DIM],
-                        in0=v_rows[:, head // GROUP, dims],
-                        scalar=factor[:, head * TILES + i : head * TILES + i + 1],
-                        in1=a_rows[:, head, dims],
-                        op0=ALU.mult,
-                        op1=ALU.add,
-                    )
-                turned = turned_banks.tile([P, PASSES, PAIR, P], F32, tag="turned")
-                for c in range(PASSES):
-                    transpose_words(
-                        nc,
-                        [turned[:, c, u, :] for u in range(PAIR)],
-                        y_words[:, i, c * WORDS_PASS : (c + 1) * WORDS_PASS],
-                        identity[:],
-                    )
-                turned_of[chunk].append(turned)
+        def narrow_passes(i):
+            return [c for c in range(PASSES) if (i, c) != (WIDE_TILE, WIDE_PASS)]
 
-        def regroup(chunk, part):
-            grouped = parts.tile([P, PASSES, PART_TILES, P, PACK], BF16, align_bytes=64)
-            grouped_words = grouped[:].bitcast(F32)
-            for j in range(PART_TILES):
-                nc.scalar.copy(
-                    out=grouped_words[:, :, j],
-                    in_=turned_of[chunk][part * PART_TILES + j][:].rearrange("p c u t -> p c t u"),
+        def heads_of(c):
+            return range(c * PASS_HEADS, (c + 1) * PASS_HEADS)
+
+        def project(chunk, i):
+            dims = slice(i * HEAD_DIM, (i + 1) * HEAD_DIM)
+            y = parts.tile([P, K], BF16)
+            for head in [head for c in narrow_passes(i) for head in heads_of(c)]:
+                nc.vector.scalar_tensor_tensor(
+                    out=y[:, head * HEAD_DIM : (head + 1) * HEAD_DIM],
+                    in0=v_of[chunk][:, head // GROUP, dims],
+                    scalar=factor_of[chunk][:, head * TILES + i : head * TILES + i + 1],
+                    in1=a_of[chunk][:, head, dims],
+                    op0=ALU.mult,
+                    op1=ALU.add,
                 )
-            grouped_of[chunk, part] = grouped
+            y_of[chunk, i] = y
+
+        def turn(chunk, i):
+            y_words = y_of[chunk, i][:].bitcast(F32)
+            turned = turned_banks.tile([P, PASSES, PAIR, P], F32, tag="turned")
+            for c in narrow_passes(i):
+                transpose_words(
+                    nc,
+                    [turned[:, c, u, :] for u in range(PAIR)],
+                    y_words[:, c * WORDS_PASS : (c + 1) * WORDS_PASS],
+                    identity[:],
+                )
+            turned_of[chunk, i] = turned
+
+        wide_dims = slice(WIDE_TILE * HEAD_DIM, (WIDE_TILE + 1) * HEAD_DIM)
+        wide_heads = heads_of(WIDE_PASS)
+
+        def widen_a(chunk):
+            wide_a = work.tile([P, PASS_HEADS, HEAD_DIM], F32)
+            nc.scalar.copy(
+                out=wide_a[:], in_=a_of[chunk][:, wide_heads.start : wide_heads.stop, wide_dims]
+            )
+            wide_a_of[chunk] = wide_a
+
+        def scale_v(chunk):
+            wide_w = work.tile([P, PASS_HEADS, HEAD_DIM], F32)
+            for n, head in enumerate(wide_heads):
+                unit = head * TILES + WIDE_TILE
+                nc.scalar.activation(
+                    out=wide_w[:, n, :],
+                    in_=v_of[chunk][:, head // GROUP, wide_dims],
+                    func=ACT.Copy,
+                    scale=factor_of[chunk][:, unit : unit + 1],
+                )
+            wide_w_of[chunk] = wide_w
+
+        def add_and_turn(chunk):
+            terms = [
+                wide[:].rearrange("p h d -> p (h d)") for wide in (wide_a_of[chunk], wide_w_of[chunk])
+            ]
+            wide_bank = turned_banks.tile([P, PACK, P], F32, tag="turned")
+            for t in range(PACK):
+                for n, term in enumerate(terms):
+                    nc.tensor.matmul(
+                        out=wide_bank[:, t, :],
+                        lhsT=term[:, t::PACK],
+                        rhs=identity[:],
+                        is_transpose=True,
+                        start=(n == 0),
+                        stop=(n == 1),
+                    )
+            wide_banks_of[chunk] = wide_bank
+
+        def grouped_tile(chunk, i):
+            part = part_of(chunk, i)
+            if (chunk, part) not in grouped_of:
+                n = len(parts_of(chunk)[part])
+                grouped = parts.tile([P, PASSES, n, P, PACK], BF16, align_bytes=64)
+                grouped_of[chunk, part] = grouped
+            return grouped_of[chunk, part], parts_of(chunk)[part].index(i)
+
+        def regroup(chunk, i):
+            grouped, j = grouped_tile(chunk, i)
+            passes = narrow_passes(i)
+            span = slice(passes[0], passes[-1] + 1)
+            nc.scalar.copy(
+                out=grouped[:].bitcast(F32)[:, span, j],
+                in_=turned_of[chunk, i][:, span].rearrange("p c u t -> p c t u"),
+            )
+
+        def regroup_wide(chunk):
+            grouped, j = grouped_tile(chunk, WIDE_TILE)
+            nc.scalar.copy(
+                out=grouped[:, WIDE_PASS, j], in_=wide_banks_of[chunk][:].rearrange("p t n -> p n t")
+            )
 
         def quantise(chunk, part):
-            codes = parts.tile([P, PASSES, PART], U32, align_bytes=64)
-            scales = parts.tile([P, PASSES, PART], U8, align_bytes=64)
+            width = len(parts_of(chunk)[part]) * P
+            codes = parts.tile([P, PASSES, width], U32, align_bytes=64)
+            scales = parts.tile([P, PASSES, width], U8, align_bytes=64)
             nc.vector.quantize_mx(
                 out=codes[:].rearrange("p c t -> p (c t)").bitcast(FP8X4),
                 scales=scales[:].rearrange("p c t -> p (c t)"),
@@ -263,7 +345,8 @@ def tile_block_pb_t_kernel(tc, attn_out, v, x, wo, attn_scale, out):
 
         def multiply(chunk, part):
             codes, scales = codes_of[chunk, part], scales_of[chunk, part]
-            sums = sum_banks.tile([P, HALVES, PART], F32)
+            width = len(parts_of(chunk)[part]) * P
+            sums = sum_banks.tile([P, HALVES, width], F32)
             for half in range(HALVES):
                 channels = slice(half * P, (half + 1) * P)
                 for c in range(PASSES):
@@ -279,7 +362,8 @@ def tile_block_pb_t_kernel(tc, attn_out, v, x, wo, attn_scale, out):
             sums_of[chunk, part] = sums
 
         def apply_gain(chunk, part):
-            scaled = parts.tile([P, HALVES, PART], F32)
+            width = len(parts_of(chunk)[part]) * P
+            scaled = parts.tile([P, HALVES, width], F32)
             for half in range(HALVES):
                 nc.scalar.activation(
                     out=scaled[:, half, :],
@@ -289,13 +373,11 @@ def tile_block_pb_t_kernel(tc, attn_out, v, x, wo, attn_scale, out):
                 )
             scaled_of[chunk, part] = scaled
 
-        def adds_on_tensor(chunk, part):
-            return (chunk * PARTS + part) % 4 != 3
-
         def transpose_back(chunk, part):
             scaled = scaled_of[chunk, part]
-            back = out_banks.tile([P, PART_TILES, CHANNELS], F32)
-            for j in range(PART_TILES):
+            tiles = parts_of(chunk)[part]
+            back = out_banks.tile([P, len(tiles), CHANNELS], F32)
+            for j, i in enumerate(tiles):
                 for half in range(HALVES):
                     nc.tensor.matmul(
                         out=back[:, j, half * P : (half + 1) * P],
@@ -303,10 +385,9 @@ def tile_block_pb_t_kernel(tc, attn_out, v, x, wo, attn_scale, out):
                         rhs=identity[:],
                         is_transpose=True,
                         start=(half == 0),
-                        stop=(half == HALVES - 1 and not adds_on_tensor(chunk, part)),
+                        stop=(half == HALVES - 1 and not adds_on_tensor(chunk)),
                     )
-                if adds_on_tensor(chunk, part):
-                    i = part * PART_TILES + j
+                if adds_on_tensor(chunk):
                     nc.tensor.matmul(
                         out=back[:, j, :],
                         lhsT=identity_bf16[:],
@@ -316,64 +397,94 @@ def tile_block_pb_t_kernel(tc, attn_out, v, x, wo, attn_scale, out):
                     )
             back_of[chunk, part] = back
 
-        def add_residual_and_store(chunk, part):
+        def finish(chunk, part):
             b, tokens = tokens_of(chunk)
-            result = parts.tile([P, PART_TILES, CHANNELS], F32)
-            if adds_on_tensor(chunk, part):
+            tiles = parts_of(chunk)[part]
+            span = slice(tiles[0], tiles[-1] + 1)
+            result = parts.tile([P, len(tiles), CHANNELS], F32)
+            if adds_on_tensor(chunk):
                 nc.scalar.copy(out=result[:], in_=back_of[chunk, part][:])
             else:
                 nc.vector.tensor_tensor(
                     out=result[:].rearrange("p j n -> p (j n)"),
                     in0=back_of[chunk, part][:].rearrange("p j n -> p (j n)"),
-                    in1=x_of[chunk][:, part * BANK : (part + 1) * BANK],
+                    in1=x_of[chunk][:, span.start * CHANNELS : span.stop * CHANNELS],
                     op=ALU.add,
                 )
-            queue = nc.sync if chunk == CHUNKS - 1 else nc.gpsimd
-            tiles = slice(part * PART_TILES, (part + 1) * PART_TILES)
-            queue.dma_start(
-                out=out[b, tokens, :].rearrange("(p i) n -> p i n", i=TILES)[:, tiles, :],
+            nc.sync.dma_start(
+                out=out[b, tokens, :].rearrange("(p i) n -> p i n", i=TILES)[:, span, :],
                 in_=result[:],
             )
 
         def exists(chunk):
             return 0 <= chunk < CHUNKS
 
-        load(0)
-        for step in range(CHUNKS + 3):
-            ahead, now, behind, last = step, step - 1, step - 2, step - 3
-            if exists(ahead + 1):
-                load(ahead + 1)
-            if exists(now):
-                load_residual(now)
-            if exists(behind):
-                for part in range(PARTS):
-                    regroup(behind, part)
-            if exists(ahead):
-                squared_norms(ahead)
-                multiply_elements(ahead)
-                sum_products(ahead)
-            if exists(now):
-                dot_products(now)
-            if exists(last):
-                for part in range(PARTS):
-                    add_residual_and_store(last, part)
-            if step == 1:
-                prepare_wo_and_gain()
-            if exists(now):
+        def projected_in(slot):
+            chunk, i = divmod(slot - 2 * TILES - 2, TILES)
+            return (chunk, i) if exists(chunk) else None
+
+        def part_ending_in(slot):
+            here = projected_in(slot)
+            if here is None:
+                return None
+            chunk, i = here
+            part = part_of(chunk, i)
+            return (chunk, part) if i == parts_of(chunk)[part][-1] else None
+
+        for slot in range(TILES * (CHUNKS + 2) + 9):
+            n, q = divmod(slot, TILES)
+            ahead, dots, now = n, n - 1, n - 2
+            here, before = projected_in(slot), projected_in(slot - 1)
+            quantised, multiplied = part_ending_in(slot - 2), part_ending_in(slot - 3)
+            turned_back, finished = part_ending_in(slot - 4), part_ending_in(slot - 5)
+            if q == 0:
+                if exists(ahead + 2):
+                    load(ahead + 2)
+                if exists(dots):
+                    load_residual(dots)
+            if q == 0 and exists(now):
+                copy_phase_sums(now)
+            if q == 0 and exists(now - 1):
+                regroup_wide(now - 1)
+            if finished is not None:
+                finish(*finished)
+            if q == 2 and exists(now):
                 factors(now)
             if exists(ahead):
-                floor_norms(ahead)
-            if exists(behind):
-                for part in range(PARTS):
-                    quantise(behind, part)
-                    multiply(behind, part)
+                multiply_elements(ahead, q)
+            if multiplied is not None:
+                multiply(*multiplied)
+            if q == 0 and exists(now):
+                turn_phase_sums(now)
+            if exists(dots):
+                sum_products(dots, q)
+            if before is not None:
+                turn(*before)
+            if turned_back is not None:
+                transpose_back(*turned_back)
+            if q == 2 and exists(now):
+                scale_v(now)
+            if multiplied is not None:
+                apply_gain(*multiplied)
+            if before is not None:
+                regroup(*before)
+            if q == 3 and exists(now):
+                add_and_turn(now)
             if exists(ahead):
-                invert_norms(ahead)
-            if exists(behind):
-                for part in range(PARTS):
-                    apply_gain(behind, part)
-            if exists(now):
-                project_and_transpose(now)
-            if exists(behind):
-                for part in range(PARTS):
-                    transpose_back(behind, part)
+                squared_norms(ahead, [q])
+            if q == 1 and exists(now):
+                widen_a(now)
+            if q == 0 and exists(now):
+                floor_norms(now)
+            if here is not None:
+                project(*here)
+            if q == 0 and exists(now):
+                invert_norms(now)
+            if q == 1 and exists(now):
+                dot_products(now)
+            if quantised is not None:
+                quantise(*quantised)
+            if slot == 8:
+                turn_wo_and_gain()
+            if slot == 10:
+                quantise_wo()

@@ -26,6 +26,9 @@ HALVES = CHANNELS // P
 
 TILES = 4
 CHUNKS = BATCH * SEQ // (TILES * P)
+UNITS = HEADS * TILES
+PHASES = P // UNITS
+STEPS = HEAD_DIM // PHASES
 WIDE_TILE = 0
 WIDE_PASS = 0
 PASS_HEADS = HEADS // PASSES
@@ -163,30 +166,31 @@ def tile_block_pb_t_kernel(tc, attn_out, v, x, wo, attn_scale, out):
 
         def multiply_elements(chunk, h):
             if chunk not in products_of:
-                products = inputs.tile([P, HEADS, TILES * HEAD_DIM], F32, bufs=3)
+                products = inputs.tile([P, STEPS, UNITS, PHASES], F32, bufs=3)
                 products_of[chunk] = products
             heads = slice(h * GROUP, (h + 1) * GROUP)
+            units = slice(h * GROUP * TILES, (h + 1) * GROUP * TILES)
             nc.vector.tensor_tensor(
-                out=products_of[chunk][:, heads, :],
-                in0=a_of[chunk][:, heads, :],
-                in1=v_of[chunk][:, h : h + 1, :].to_broadcast([P, GROUP, TILES * HEAD_DIM]),
+                out=products_of[chunk][:, :, units, :].rearrange("p j (g i) f -> p g i j f", g=GROUP),
+                in0=a_of[chunk][:, heads, :].rearrange("p g (i j f) -> p g i j f", i=TILES, f=PHASES),
+                in1=v_of[chunk][:, h : h + 1, :]
+                .rearrange("p o (i j f) -> p o i j f", i=TILES, f=PHASES)
+                .to_broadcast([P, GROUP, TILES, STEPS, PHASES]),
                 op=ALU.mult,
             )
 
         def sum_products(chunk, quarter):
-            step = HEADS * TILES
-            flat = products_of[chunk][:].rearrange("p h r -> p (h r)")
             if quarter == 0:
                 dot_bank = dot_banks.tile([P, 2, P], F32)
                 dot_bank_of[chunk] = dot_bank
-            for j in range(quarter * step // 4, (quarter + 1) * step // 4):
+            for j in range(quarter * STEPS // 4, (quarter + 1) * STEPS // 4):
                 nc.tensor.matmul(
                     out=dot_bank_of[chunk][:, 0, :],
-                    lhsT=flat[:, j::step],
+                    lhsT=products_of[chunk][:, j].rearrange("p u f -> p (u f)"),
                     rhs=identity[:],
                     is_transpose=True,
                     start=(j == 0),
-                    stop=(j == step - 1),
+                    stop=(j == STEPS - 1),
                 )
 
         phase_sums_of = {}
@@ -274,34 +278,35 @@ def tile_block_pb_t_kernel(tc, attn_out, v, x, wo, attn_scale, out):
         wide_heads = heads_of(WIDE_PASS)
 
         def widen_a(chunk):
-            wide_a = work.tile([P, PASS_HEADS, HEAD_DIM], F32)
+            wide_a = work.tile([P, PACK, PASS_HEADS, HEAD_DIM // PACK], F32)
             nc.scalar.copy(
-                out=wide_a[:], in_=a_of[chunk][:, wide_heads.start : wide_heads.stop, wide_dims]
+                out=wide_a[:],
+                in_=a_of[chunk][:, wide_heads.start : wide_heads.stop, wide_dims].rearrange(
+                    "p h (q t) -> p t h q", t=PACK
+                ),
             )
             wide_a_of[chunk] = wide_a
 
         def scale_v(chunk):
-            wide_w = work.tile([P, PASS_HEADS, HEAD_DIM], F32)
+            wide_w = work.tile([P, PACK, PASS_HEADS, HEAD_DIM // PACK], F32)
             for n, head in enumerate(wide_heads):
                 unit = head * TILES + WIDE_TILE
                 nc.scalar.activation(
-                    out=wide_w[:, n, :],
-                    in_=v_of[chunk][:, head // GROUP, wide_dims],
+                    out=wide_w[:, :, n, :],
+                    in_=v_of[chunk][:, head // GROUP, wide_dims].rearrange("p (q t) -> p t q", t=PACK),
                     func=ACT.Copy,
                     scale=factor_of[chunk][:, unit : unit + 1],
                 )
             wide_w_of[chunk] = wide_w
 
         def add_and_turn(chunk):
-            terms = [
-                wide[:].rearrange("p h d -> p (h d)") for wide in (wide_a_of[chunk], wide_w_of[chunk])
-            ]
+            terms = [wide_a_of[chunk], wide_w_of[chunk]]
             wide_bank = turned_banks.tile([P, PACK, P], F32, tag="turned")
             for t in range(PACK):
                 for n, term in enumerate(terms):
                     nc.tensor.matmul(
                         out=wide_bank[:, t, :],
-                        lhsT=term[:, t::PACK],
+                        lhsT=term[:, t].rearrange("p h q -> p (h q)"),
                         rhs=identity[:],
                         is_transpose=True,
                         start=(n == 0),

@@ -30,9 +30,9 @@ UNITS = HEADS * TILES
 PHASES = P // UNITS
 STEPS = HEAD_DIM // PHASES
 WIDE_TILE = 0
-WIDE_PASS = 0
+WIDE_PASSES = [[0, 1]] * 5 + [[0], [0], [0]]
 PASS_HEADS = HEADS // PASSES
-TENSOR_RESIDUAL_CHUNKS = 6
+VECTOR_RESIDUAL_CHUNKS = 2
 
 NORM_FLOOR_SQUARED = 1e-24
 
@@ -76,7 +76,7 @@ def tile_block_pb_t_kernel(tc, attn_out, v, x, wo, attn_scale, out):
             return [i in tiles for tiles in parts_of(chunk)].index(True)
 
         def adds_on_tensor(chunk):
-            return chunk < TENSOR_RESIDUAL_CHUNKS
+            return chunk >= VECTOR_RESIDUAL_CHUNKS
 
         def load(chunk):
             b, tokens = tokens_of(chunk)
@@ -242,8 +242,8 @@ def tile_block_pb_t_kernel(tc, attn_out, v, x, wo, attn_scale, out):
             )
             factor_of[chunk] = factor
 
-        def narrow_passes(i):
-            return [c for c in range(PASSES) if (i, c) != (WIDE_TILE, WIDE_PASS)]
+        def narrow_passes(chunk, i):
+            return [c for c in range(PASSES) if i != WIDE_TILE or c not in WIDE_PASSES[chunk]]
 
         def heads_of(c):
             return range(c * PASS_HEADS, (c + 1) * PASS_HEADS)
@@ -251,7 +251,7 @@ def tile_block_pb_t_kernel(tc, attn_out, v, x, wo, attn_scale, out):
         def project(chunk, i):
             dims = slice(i * HEAD_DIM, (i + 1) * HEAD_DIM)
             y = parts.tile([P, K], BF16)
-            for head in [head for c in narrow_passes(i) for head in heads_of(c)]:
+            for head in [head for c in narrow_passes(chunk, i) for head in heads_of(c)]:
                 nc.vector.scalar_tensor_tensor(
                     out=y[:, head * HEAD_DIM : (head + 1) * HEAD_DIM],
                     in0=v_of[chunk][:, head // GROUP, dims],
@@ -265,7 +265,7 @@ def tile_block_pb_t_kernel(tc, attn_out, v, x, wo, attn_scale, out):
         def turn(chunk, i):
             y_words = y_of[chunk, i][:].bitcast(F32)
             turned = turned_banks.tile([P, PASSES, PAIR, P], F32, tag="turned")
-            for c in narrow_passes(i):
+            for c in narrow_passes(chunk, i):
                 transpose_words(
                     nc,
                     [turned[:, c, u, :] for u in range(PAIR)],
@@ -275,21 +275,20 @@ def tile_block_pb_t_kernel(tc, attn_out, v, x, wo, attn_scale, out):
             turned_of[chunk, i] = turned
 
         wide_dims = slice(WIDE_TILE * HEAD_DIM, (WIDE_TILE + 1) * HEAD_DIM)
-        wide_heads = heads_of(WIDE_PASS)
 
-        def widen_a(chunk):
+        def widen_a(chunk, c):
             wide_a = work.tile([P, PACK, PASS_HEADS, HEAD_DIM // PACK], F32)
             nc.scalar.copy(
                 out=wide_a[:],
-                in_=a_of[chunk][:, wide_heads.start : wide_heads.stop, wide_dims].rearrange(
+                in_=a_of[chunk][:, heads_of(c).start : heads_of(c).stop, wide_dims].rearrange(
                     "p h (q t) -> p t h q", t=PACK
                 ),
             )
-            wide_a_of[chunk] = wide_a
+            wide_a_of[chunk, c] = wide_a
 
-        def scale_v(chunk):
+        def scale_v(chunk, c):
             wide_w = work.tile([P, PACK, PASS_HEADS, HEAD_DIM // PACK], F32)
-            for n, head in enumerate(wide_heads):
+            for n, head in enumerate(heads_of(c)):
                 unit = head * TILES + WIDE_TILE
                 nc.scalar.activation(
                     out=wide_w[:, :, n, :],
@@ -297,10 +296,10 @@ def tile_block_pb_t_kernel(tc, attn_out, v, x, wo, attn_scale, out):
                     func=ACT.Copy,
                     scale=factor_of[chunk][:, unit : unit + 1],
                 )
-            wide_w_of[chunk] = wide_w
+            wide_w_of[chunk, c] = wide_w
 
-        def add_and_turn(chunk):
-            terms = [wide_a_of[chunk], wide_w_of[chunk]]
+        def add_and_turn(chunk, c):
+            terms = [wide_a_of[chunk, c], wide_w_of[chunk, c]]
             wide_bank = turned_banks.tile([P, PACK, P], F32, tag="turned")
             for t in range(PACK):
                 for n, term in enumerate(terms):
@@ -312,7 +311,7 @@ def tile_block_pb_t_kernel(tc, attn_out, v, x, wo, attn_scale, out):
                         start=(n == 0),
                         stop=(n == 1),
                     )
-            wide_banks_of[chunk] = wide_bank
+            wide_banks_of[chunk, c] = wide_bank
 
         def grouped_tile(chunk, i):
             part = part_of(chunk, i)
@@ -324,17 +323,17 @@ def tile_block_pb_t_kernel(tc, attn_out, v, x, wo, attn_scale, out):
 
         def regroup(chunk, i):
             grouped, j = grouped_tile(chunk, i)
-            passes = narrow_passes(i)
+            passes = narrow_passes(chunk, i)
             span = slice(passes[0], passes[-1] + 1)
             nc.scalar.copy(
                 out=grouped[:].bitcast(F32)[:, span, j],
                 in_=turned_of[chunk, i][:, span].rearrange("p c u t -> p c t u"),
             )
 
-        def regroup_wide(chunk):
+        def regroup_wide(chunk, c):
             grouped, j = grouped_tile(chunk, WIDE_TILE)
             nc.scalar.copy(
-                out=grouped[:, WIDE_PASS, j], in_=wide_banks_of[chunk][:].rearrange("p t n -> p n t")
+                out=grouped[:, c, j], in_=wide_banks_of[chunk, c][:].rearrange("p t n -> p n t")
             )
 
         def quantise(chunk, part):
@@ -436,12 +435,23 @@ def tile_block_pb_t_kernel(tc, attn_out, v, x, wo, attn_scale, out):
             part = part_of(chunk, i)
             return (chunk, part) if i == parts_of(chunk)[part][-1] else None
 
-        for slot in range(TILES * (CHUNKS + 2) + 9):
+        def part_quantised_in(slot):
+            for lag in (2, 3):
+                ending = part_ending_in(slot - lag)
+                if ending is not None and lag == (3 if ending[0] in (5, 6) else 2):
+                    return ending
+            return None
+
+        for slot in range(TILES * (CHUNKS + 2) + 11):
             n, q = divmod(slot, TILES)
             ahead, dots, now = n, n - 1, n - 2
             here, before = projected_in(slot), projected_in(slot - 1)
-            quantised, multiplied = part_ending_in(slot - 2), part_ending_in(slot - 3)
-            turned_back, finished = part_ending_in(slot - 4), part_ending_in(slot - 5)
+            if before is not None and not narrow_passes(*before):
+                before = None
+            if here is not None and not narrow_passes(*here):
+                here = None
+            quantised, multiplied = part_quantised_in(slot), part_quantised_in(slot - 1)
+            turned_back, finished = part_quantised_in(slot - 2), part_quantised_in(slot - 3)
             if q == 0:
                 if exists(ahead + 2):
                     load(ahead + 2)
@@ -450,35 +460,39 @@ def tile_block_pb_t_kernel(tc, attn_out, v, x, wo, attn_scale, out):
             if q == 0 and exists(now):
                 copy_phase_sums(now)
             if q == 0 and exists(now - 1):
-                regroup_wide(now - 1)
+                for c in WIDE_PASSES[now - 1]:
+                    regroup_wide(now - 1, c)
             if finished is not None:
                 finish(*finished)
             if q == 2 and exists(now):
                 factors(now)
             if exists(ahead):
                 multiply_elements(ahead, q)
+            if before is not None:
+                turn(*before)
             if multiplied is not None:
                 multiply(*multiplied)
             if q == 0 and exists(now):
                 turn_phase_sums(now)
             if exists(dots):
                 sum_products(dots, q)
-            if before is not None:
-                turn(*before)
             if turned_back is not None:
                 transpose_back(*turned_back)
             if q == 2 and exists(now):
-                scale_v(now)
+                for c in WIDE_PASSES[now]:
+                    scale_v(now, c)
             if multiplied is not None:
                 apply_gain(*multiplied)
             if before is not None:
                 regroup(*before)
             if q == 3 and exists(now):
-                add_and_turn(now)
+                for c in WIDE_PASSES[now]:
+                    add_and_turn(now, c)
             if exists(ahead):
                 squared_norms(ahead, [q])
             if q == 1 and exists(now):
-                widen_a(now)
+                for c in WIDE_PASSES[now]:
+                    widen_a(now, c)
             if q == 0 and exists(now):
                 floor_norms(now)
             if here is not None:

@@ -41,7 +41,7 @@ FLOPS = 2 * BATCH * SEQ * K * CHANNELS
 
 def transpose_words(nc, turned_halves, words, identity):
     for u in range(PAIR):
-        nc.tensor.transpose(turned_halves[u], words[:, u:WORDS_PASS:PAIR], identity)
+        nc.tensor.transpose(turned_halves[u], words[:, u * P : (u + 1) * P], identity)
 
 
 def tile_block_pb_t_kernel(tc, attn_out, v, x, wo, attn_scale, out):
@@ -277,22 +277,24 @@ def tile_block_pb_t_kernel(tc, attn_out, v, x, wo, attn_scale, out):
         wide_dims = slice(WIDE_TILE * HEAD_DIM, (WIDE_TILE + 1) * HEAD_DIM)
 
         def widen_a(chunk, c):
-            wide_a = work.tile([P, PACK, PASS_HEADS, HEAD_DIM // PACK], F32)
-            nc.scalar.copy(
-                out=wide_a[:],
-                in_=a_of[chunk][:, heads_of(c).start : heads_of(c).stop, wide_dims].rearrange(
-                    "p h (q t) -> p t h q", t=PACK
-                ),
-            )
+            wide_a = work.tile([P, PAIR, PAIR, GROUP, HEAD_DIM // PAIR], F32)
+            for u in range(PAIR):
+                first = heads_of(c).start + u * GROUP
+                nc.scalar.copy(
+                    out=wide_a[:, u],
+                    in_=a_of[chunk][:, first : first + GROUP, wide_dims].rearrange(
+                        "p g (q e) -> p e g q", e=PAIR
+                    ),
+                )
             wide_a_of[chunk, c] = wide_a
 
         def scale_v(chunk, c):
-            wide_w = work.tile([P, PACK, PASS_HEADS, HEAD_DIM // PACK], F32)
+            wide_w = work.tile([P, PAIR, PAIR, GROUP, HEAD_DIM // PAIR], F32)
             for n, head in enumerate(heads_of(c)):
                 unit = head * TILES + WIDE_TILE
                 nc.scalar.activation(
-                    out=wide_w[:, :, n, :],
-                    in_=v_of[chunk][:, head // GROUP, wide_dims].rearrange("p (q t) -> p t q", t=PACK),
+                    out=wide_w[:, n // GROUP, :, n % GROUP, :],
+                    in_=v_of[chunk][:, head // GROUP, wide_dims].rearrange("p (q e) -> p e q", e=PAIR),
                     func=ACT.Copy,
                     scale=factor_of[chunk][:, unit : unit + 1],
                 )
@@ -305,7 +307,7 @@ def tile_block_pb_t_kernel(tc, attn_out, v, x, wo, attn_scale, out):
                 for n, term in enumerate(terms):
                     nc.tensor.matmul(
                         out=wide_bank[:, t, :],
-                        lhsT=term[:, t].rearrange("p h q -> p (h q)"),
+                        lhsT=term[:, t // PAIR, t % PAIR].rearrange("p g q -> p (g q)"),
                         rhs=identity[:],
                         is_transpose=True,
                         start=(n == 0),

@@ -30,7 +30,7 @@ UNITS = HEADS * TILES
 PHASES = P // UNITS
 STEPS = HEAD_DIM // PHASES
 WIDE_TILE = 0
-WIDE_PASSES = [[0, 1]] * 5 + [[0], [0], [0]]
+WIDE_PASSES = [[0, 1]] * 4 + [[0]] * 4
 PASS_HEADS = HEADS // PASSES
 VECTOR_RESIDUAL_CHUNKS = 2
 
@@ -76,7 +76,7 @@ def tile_block_pb_t_kernel(tc, attn_out, v, x, wo, attn_scale, out):
             return [i in tiles for tiles in parts_of(chunk)].index(True)
 
         def adds_on_tensor(chunk):
-            return chunk >= VECTOR_RESIDUAL_CHUNKS
+            return 0 < chunk < CHUNKS - 1
 
         def load(chunk):
             b, tokens = tokens_of(chunk)
@@ -101,13 +101,13 @@ def tile_block_pb_t_kernel(tc, attn_out, v, x, wo, attn_scale, out):
             )
             x_of[chunk] = x_rows
 
-        load(0)
-        load(1)
         wo_rows = const.tile([P, HALVES, K], BF16)
-        nc.sync.dma_start(out=wo_rows[:], in_=wo.rearrange("(half p) k -> p half k", p=P))
         gain_rows = const.tile([P, CHANNELS], BF16)
         nc.gpsimd.memset(gain_rows[:], 0.0)
-        nc.sync.dma_start(out=gain_rows[0:1, :], in_=attn_scale.rearrange("(o n) -> o n", o=1))
+
+        def load_wo_and_gain():
+            nc.sync.dma_start(out=wo_rows[:], in_=wo.rearrange("(half p) k -> p half k", p=P))
+            nc.sync.dma_start(out=gain_rows[0:1, :], in_=attn_scale.rearrange("(o n) -> o n", o=1))
 
         identity = const.tile([P, P], F32)
         make_identity(nc, identity[:])
@@ -454,17 +454,21 @@ def tile_block_pb_t_kernel(tc, attn_out, v, x, wo, attn_scale, out):
                 here = None
             quantised, multiplied = part_quantised_in(slot), part_quantised_in(slot - 1)
             turned_back, finished = part_quantised_in(slot - 2), part_quantised_in(slot - 3)
+            if slot == 0:
+                for chunk in range(3):
+                    load(chunk)
+                load_wo_and_gain()
             if q == 0:
-                if exists(ahead + 2):
-                    load(ahead + 2)
-                if exists(dots):
-                    load_residual(dots)
+                if slot > 0 and exists(ahead + 3 - 1):
+                    load(ahead + 3 - 1)
+                if exists(now):
+                    load_residual(now)
             if q == 0 and exists(now):
                 copy_phase_sums(now)
             if q == 0 and exists(now - 1):
                 for c in WIDE_PASSES[now - 1]:
                     regroup_wide(now - 1, c)
-            if finished is not None:
+            if finished is not None and finished[0] < CHUNKS - 1:
                 finish(*finished)
             if q == 2 and exists(now):
                 factors(now)
@@ -505,7 +509,9 @@ def tile_block_pb_t_kernel(tc, attn_out, v, x, wo, attn_scale, out):
                 dot_products(now)
             if quantised is not None:
                 quantise(*quantised)
-            if slot == 8:
+            if finished is not None and finished[0] == CHUNKS - 1:
+                finish(*finished)
+            if slot == 12:
                 turn_wo_and_gain()
-            if slot == 10:
+            if slot == 13:
                 quantise_wo()

@@ -30,10 +30,11 @@ UNITS = HEADS * TILES
 PHASES = P // UNITS
 STEPS = HEAD_DIM // PHASES
 WIDE_TILE = 0
-WIDE_PASSES = [[0, 1]] * 4 + [[0]] * 4
+WIDE_PASSES = [[0, 1]] * 4 + [[0]] * 3 + [[]]
 PASS_HEADS = HEADS // PASSES
 VECTOR_RESIDUAL_CHUNKS = 2
 
+FINE_CHUNKS = 5
 NORM_FLOOR_SQUARED = 1e-24
 
 FLOPS = 2 * BATCH * SEQ * K * CHANNELS
@@ -82,7 +83,16 @@ def tile_block_pb_t_kernel(tc, attn_out, v, x, wo, attn_scale, out):
             b, tokens = tokens_of(chunk)
             v_rows = inputs.tile([P, KV_HEADS, TILES * HEAD_DIM], BF16)
             a_rows = inputs.tile([P, HEADS, TILES * HEAD_DIM], BF16)
-            for h in range(KV_HEADS):
+            if chunk >= FINE_CHUNKS:
+                nc.sync.dma_start(
+                    out=v_rows[:],
+                    in_=v[b, :, tokens, :].rearrange("h (p i) d -> p h (i d)", i=TILES),
+                )
+                nc.sync.dma_start(
+                    out=a_rows[:],
+                    in_=attn_out[b, :, :, tokens, :].rearrange("h g (p i) d -> p (h g) (i d)", i=TILES),
+                )
+            for h in range(KV_HEADS if chunk < FINE_CHUNKS else 0):
                 nc.sync.dma_start(
                     out=v_rows[:, h, :],
                     in_=v[b, h, tokens, :].rearrange("(p i) d -> p (i d)", i=TILES),
@@ -112,6 +122,12 @@ def tile_block_pb_t_kernel(tc, attn_out, v, x, wo, attn_scale, out):
         identity = const.tile([P, P], F32)
         make_identity(nc, identity[:])
         identity_bf16 = const.tile([P, P], BF16)
+        by_phase = const.tile([P, 2 * PHASES, UNITS], F32)
+        for copy in range(2):
+            nc.vector.tensor_copy(
+                out=by_phase[:, copy * PHASES : (copy + 1) * PHASES],
+                in_=identity[:].rearrange("p (u f) -> p f u", f=PHASES),
+            )
 
         wo_grouped = const.tile([P, PASSES, CHANNELS, PACK], BF16, align_bytes=64)
         wo_codes = const.tile([P, PASSES, CHANNELS], U32, align_bytes=64)
@@ -200,18 +216,16 @@ def tile_block_pb_t_kernel(tc, attn_out, v, x, wo, attn_scale, out):
             nc.scalar.copy(out=phase_sums[:], in_=dot_bank_of[chunk][:, 0, :])
             phase_sums_of[chunk] = phase_sums
 
-        def turn_phase_sums(chunk):
-            nc.tensor.transpose(dot_bank_of[chunk][:, 1, :], phase_sums_of[chunk][:], identity[:])
-
-        def dot_products(chunk):
-            units = HEADS * TILES
-            dot = small.tile([P, units], F32)
-            nc.vector.reduce_sum(
-                out=dot[:],
-                in_=dot_bank_of[chunk][:, 1, :].rearrange("p (u f) -> p u f", f=P // units),
-                axis=mybir.AxisListType.X,
-            )
-            dot_of[chunk] = dot
+        def add_phases(chunk):
+            for f in range(PHASES):
+                nc.tensor.matmul(
+                    out=dot_bank_of[chunk][:, 1, :],
+                    lhsT=phase_sums_of[chunk][:],
+                    rhs=by_phase[:, f : f + PHASES].rearrange("p f u -> p (f u)"),
+                    is_transpose=True,
+                    start=(f == 0),
+                    stop=(f == PHASES - 1),
+                )
 
         def floor_norms(chunk):
             floored = small.tile([P, KV_HEADS * TILES], F32)
@@ -236,7 +250,7 @@ def tile_block_pb_t_kernel(tc, attn_out, v, x, wo, attn_scale, out):
             factor = small.tile([P, HEADS * TILES], F32)
             nc.vector.tensor_tensor(
                 out=factor[:].rearrange("p (h g i) -> p h g i", g=GROUP, i=TILES),
-                in0=dot_of[chunk][:].rearrange("p (h g i) -> p h g i", g=GROUP, i=TILES),
+                in0=dot_bank_of[chunk][:, 1, :UNITS].rearrange("p (h g i) -> p h g i", g=GROUP, i=TILES),
                 in1=inverse_of[chunk][:].unsqueeze(2).to_broadcast([P, KV_HEADS, GROUP, TILES]),
                 op=ALU.mult,
             )
@@ -470,8 +484,6 @@ def tile_block_pb_t_kernel(tc, attn_out, v, x, wo, attn_scale, out):
                     regroup_wide(now - 1, c)
             if finished is not None and finished[0] < CHUNKS - 1:
                 finish(*finished)
-            if q == 2 and exists(now):
-                factors(now)
             if exists(ahead):
                 multiply_elements(ahead, q)
             if before is not None:
@@ -479,7 +491,7 @@ def tile_block_pb_t_kernel(tc, attn_out, v, x, wo, attn_scale, out):
             if multiplied is not None:
                 multiply(*multiplied)
             if q == 0 and exists(now):
-                turn_phase_sums(now)
+                add_phases(now)
             if exists(dots):
                 sum_products(dots, q)
             if turned_back is not None:
@@ -506,7 +518,7 @@ def tile_block_pb_t_kernel(tc, attn_out, v, x, wo, attn_scale, out):
             if q == 0 and exists(now):
                 invert_norms(now)
             if q == 1 and exists(now):
-                dot_products(now)
+                factors(now)
             if quantised is not None:
                 quantise(*quantised)
             if finished is not None and finished[0] == CHUNKS - 1:

from contextlib import ExitStack

import concourse.mybir as mybir
from concourse.masks import make_identity

BF16 = mybir.dt.bfloat16
F32 = mybir.dt.float32
U32 = mybir.dt.uint32
U8 = mybir.dt.uint8
FP8X4 = mybir.dt.float8_e4m3fn_x4
ALU = mybir.AluOpType
ACT = mybir.ActivationFunctionType

BATCH, SEQ, CHANNELS = 2, 2048, 256
KV_HEADS, GROUP, HEAD_DIM = 4, 2, 128
HEADS = KV_HEADS * GROUP
K = HEADS * HEAD_DIM

P = 128
PACK = 4
K_PASS = P * PACK
PASSES = K // K_PASS
PAIR = 2
WORDS_PASS = K_PASS // PAIR
HALVES = CHANNELS // P

TILES = 4
CHUNKS = BATCH * SEQ // (TILES * P)
UNITS = HEADS * TILES
PHASES = P // UNITS
STEPS = HEAD_DIM // PHASES
WIDE_TILE = 0
WIDE_PASSES = [[0, 1]] * 4 + [[0]] * 3 + [[]]
PASS_HEADS = HEADS // PASSES
VECTOR_RESIDUAL_CHUNKS = 2

FINE_CHUNKS = 5
NORM_FLOOR_SQUARED = 1e-24

FLOPS = 2 * BATCH * SEQ * K * CHANNELS


def transpose_words(nc, turned_halves, words, identity):
    for u in range(PAIR):
        nc.tensor.transpose(turned_halves[u], words[:, u * P : (u + 1) * P], identity)


def tile_block_pb_t_kernel(tc, attn_out, v, x, wo, attn_scale, out):
    nc = tc.nc
    with ExitStack() as scope:
        const = scope.enter_context(tc.tile_pool(name="const", bufs=1))
        inputs = scope.enter_context(tc.tile_pool(name="inputs", bufs=6))
        work = scope.enter_context(tc.tile_pool(name="work", bufs=2))
        parts = scope.enter_context(tc.tile_pool(name="parts", bufs=4))
        small = scope.enter_context(tc.tile_pool(name="small", bufs=3))
        turned_banks = scope.enter_context(tc.psum_pool(name="turned_banks", bufs=3))
        dot_banks = scope.enter_context(tc.psum_pool(name="dot_banks", bufs=2))
        sum_banks = scope.enter_context(tc.psum_pool(name="sum_banks", bufs=1))
        out_banks = scope.enter_context(tc.psum_pool(name="out_banks", bufs=2))
        scope.enter_context(tc.manual_schedule())

        a_of, v_of, x_of = {}, {}, {}
        norm2_of, floored_of, inverse_of, dot_of, factor_of = {}, {}, {}, {}, {}
        products_of, dot_bank_of = {}, {}
        wide_a_of, wide_w_of, y_of = {}, {}, {}
        turned_of, wide_banks_of, grouped_of, codes_of, scales_of = {}, {}, {}, {}, {}
        sums_of, scaled_of, back_of = {}, {}, {}

        def tokens_of(chunk):
            b, first = divmod(chunk * TILES * P, SEQ)
            return b, slice(first, first + TILES * P)

        def parts_of(chunk):
            return [[0, 1], [2], [3]] if chunk == CHUNKS - 1 else [[0, 1], [2, 3]]

        def part_of(chunk, i):
            return [i in tiles for tiles in parts_of(chunk)].index(True)

        def adds_on_tensor(chunk):
            return 0 < chunk < CHUNKS - 1

        def load(chunk):
            b, tokens = tokens_of(chunk)
            v_rows = inputs.tile([P, KV_HEADS, TILES * HEAD_DIM], BF16)
            a_rows = inputs.tile([P, HEADS, TILES * HEAD_DIM], BF16)
            if chunk >= FINE_CHUNKS:
                nc.sync.dma_start(
                    out=v_rows[:],
                    in_=v[b, :, tokens, :].rearrange("h (p i) d -> p h (i d)", i=TILES),
                )
                nc.sync.dma_start(
                    out=a_rows[:],
                    in_=attn_out[b, :, :, tokens, :].rearrange("h g (p i) d -> p (h g) (i d)", i=TILES),
                )
            for h in range(KV_HEADS if chunk < FINE_CHUNKS else 0):
                nc.sync.dma_start(
                    out=v_rows[:, h, :],
                    in_=v[b, h, tokens, :].rearrange("(p i) d -> p (i d)", i=TILES),
                )
                nc.sync.dma_start(
                    out=a_rows[:, h * GROUP : (h + 1) * GROUP, :],
                    in_=attn_out[b, h, :, tokens, :].rearrange("g (p i) d -> p g (i d)", i=TILES),
                )
            a_of[chunk], v_of[chunk] = a_rows, v_rows

        def load_residual(chunk):
            b, tokens = tokens_of(chunk)
            x_rows = inputs.tile([P, TILES * CHANNELS], BF16)
            nc.sync.dma_start(
                out=x_rows[:], in_=x[b, tokens, :].rearrange("(p i) n -> p (i n)", i=TILES)
            )
            x_of[chunk] = x_rows

        wo_rows = const.tile([P, HALVES, K], BF16)
        gain_rows = const.tile([P, CHANNELS], BF16)
        nc.gpsimd.memset(gain_rows[:], 0.0)

        def load_wo_and_gain():
            nc.sync.dma_start(out=wo_rows[:], in_=wo.rearrange("(half p) k -> p half k", p=P))
            nc.sync.dma_start(out=gain_rows[0:1, :], in_=attn_scale.rearrange("(o n) -> o n", o=1))

        identity = const.tile([P, P], F32)
        make_identity(nc, identity[:])
        identity_bf16 = const.tile([P, P], BF16)
        by_phase = const.tile([P, 2 * PHASES, UNITS], F32)
        for copy in range(2):
            nc.vector.tensor_copy(
                out=by_phase[:, copy * PHASES : (copy + 1) * PHASES],
                in_=identity[:].rearrange("p (u f) -> p f u", f=PHASES),
            )

        wo_grouped = const.tile([P, PASSES, CHANNELS, PACK], BF16, align_bytes=64)
        wo_codes = const.tile([P, PASSES, CHANNELS], U32, align_bytes=64)
        wo_scales = const.tile([P, PASSES, CHANNELS], U8, align_bytes=64)
        gain_column = const.tile([P, HALVES], F32)

        def turn_wo_and_gain():
            wo_words = wo_rows[:].bitcast(F32)
            grouped_words = wo_grouped[:].bitcast(F32)
            nc.scalar.copy(out=identity_bf16[:], in_=identity[:])
            for c in range(PASSES):
                turned = turned_banks.tile([P, PAIR, CHANNELS], F32, tag="turned")
                for half in range(HALVES):
                    transpose_words(
                        nc,
                        [turned[:, u, half * P : (half + 1) * P] for u in range(PAIR)],
                        wo_words[:, half, c * WORDS_PASS : (c + 1) * WORDS_PASS],
                        identity[:],
                    )
                nc.scalar.copy(out=grouped_words[:, c], in_=turned[:].rearrange("p u n -> p n u"))
            gain_wide = const.tile([P, CHANNELS], F32)
            nc.scalar.copy(out=gain_wide[:], in_=gain_rows[:])
            turned = turned_banks.tile([P, HALVES, P], F32, tag="turned")
            for half in range(HALVES):
                nc.tensor.transpose(
                    turned[:, half, :], gain_wide[:, half * P : (half + 1) * P], identity[:]
                )
            nc.scalar.copy(out=gain_column[:], in_=turned[:, :, 0])

        def quantise_wo():
            nc.vector.quantize_mx(
                out=wo_codes[:].rearrange("p c n -> p (c n)").bitcast(FP8X4),
                scales=wo_scales[:].rearrange("p c n -> p (c n)"),
                in_=wo_grouped[:].rearrange("p c n k -> p (c n k)"),
            )

        def squared_norms(chunk, kv_heads):
            if chunk not in norm2_of:
                norm2 = small.tile([P, KV_HEADS * TILES], F32)
                squares_unread = work.tile([P, KV_HEADS, TILES * HEAD_DIM], BF16)
                norm2_of[chunk] = (norm2, squares_unread)
            norm2, squares_unread = norm2_of[chunk]
            for h in kv_heads:
                for i in range(TILES):
                    dims = slice(i * HEAD_DIM, (i + 1) * HEAD_DIM)
                    nc.scalar.activation(
                        out=squares_unread[:, h, dims],
                        in_=v_of[chunk][:, h, dims],
                        func=ACT.Square,
                        accum_out=norm2[:, h * TILES + i : h * TILES + i + 1],
                    )

        def multiply_elements(chunk, h):
            if chunk not in products_of:
                products = inputs.tile([P, STEPS, UNITS, PHASES], F32, bufs=3)
                products_of[chunk] = products
            heads = slice(h * GROUP, (h + 1) * GROUP)
            units = slice(h * GROUP * TILES, (h + 1) * GROUP * TILES)
            nc.vector.tensor_tensor(
                out=products_of[chunk][:, :, units, :].rearrange("p j (g i) f -> p g i j f", g=GROUP),
                in0=a_of[chunk][:, heads, :].rearrange("p g (i j f) -> p g i j f", i=TILES, f=PHASES),
                in1=v_of[chunk][:, h : h + 1, :]
                .rearrange("p o (i j f) -> p o i j f", i=TILES, f=PHASES)
                .to_broadcast([P, GROUP, TILES, STEPS, PHASES]),
                op=ALU.mult,
            )

        def sum_products(chunk, quarter):
            if quarter == 0:
                dot_bank = dot_banks.tile([P, 2, P], F32)
                dot_bank_of[chunk] = dot_bank
            for j in range(quarter * STEPS // 4, (quarter + 1) * STEPS // 4):
                nc.tensor.matmul(
                    out=dot_bank_of[chunk][:, 0, :],
                    lhsT=products_of[chunk][:, j].rearrange("p u f -> p (u f)"),
                    rhs=identity[:],
                    is_transpose=True,
                    start=(j == 0),
                    stop=(j == STEPS - 1),
                )

        phase_sums_of = {}

        def copy_phase_sums(chunk):
            phase_sums = small.tile([P, P], F32)
            nc.scalar.copy(out=phase_sums[:], in_=dot_bank_of[chunk][:, 0, :])
            phase_sums_of[chunk] = phase_sums

        def add_phases(chunk):
            for f in range(PHASES):
                nc.tensor.matmul(
                    out=dot_bank_of[chunk][:, 1, :],
                    lhsT=phase_sums_of[chunk][:],
                    rhs=by_phase[:, f : f + PHASES].rearrange("p f u -> p (f u)"),
                    is_transpose=True,
                    start=(f == 0),
                    stop=(f == PHASES - 1),
                )

        def floor_norms(chunk):
            floored = small.tile([P, KV_HEADS * TILES], F32)
            nc.vector.tensor_scalar(
                out=floored[:],
                in0=norm2_of[chunk][0][:],
                scalar1=-1.0,
                scalar2=-NORM_FLOOR_SQUARED,
                op0=ALU.mult,
                op1=ALU.min,
            )
            floored_of[chunk] = floored

        def invert_norms(chunk):
            inverse = small.tile([P, KV_HEADS, TILES], F32)
            nc.vector.reciprocal(
                out=inverse[:].rearrange("p h i -> p (h i)"), in_=floored_of[chunk][:]
            )
            inverse_of[chunk] = inverse

        def factors(chunk):
            factor = small.tile([P, HEADS * TILES], F32)
            nc.vector.tensor_tensor(
                out=factor[:].rearrange("p (h g i) -> p h g i", g=GROUP, i=TILES),
                in0=dot_bank_of[chunk][:, 1, :UNITS].rearrange("p (h g i) -> p h g i", g=GROUP, i=TILES),
                in1=inverse_of[chunk][:].unsqueeze(2).to_broadcast([P, KV_HEADS, GROUP, TILES]),
                op=ALU.mult,
            )
            factor_of[chunk] = factor

        def narrow_passes(chunk, i):
            return [c for c in range(PASSES) if i != WIDE_TILE or c not in WIDE_PASSES[chunk]]

        def heads_of(c):
            return range(c * PASS_HEADS, (c + 1) * PASS_HEADS)

        def project(chunk, i):
            dims = slice(i * HEAD_DIM, (i + 1) * HEAD_DIM)
            y = parts.tile([P, K], BF16)
            for head in [head for c in narrow_passes(chunk, i) for head in heads_of(c)]:
                nc.vector.scalar_tensor_tensor(
                    out=y[:, head * HEAD_DIM : (head + 1) * HEAD_DIM],
                    in0=v_of[chunk][:, head // GROUP, dims],
                    scalar=factor_of[chunk][:, head * TILES + i : head * TILES + i + 1],
                    in1=a_of[chunk][:, head, dims],
                    op0=ALU.mult,
                    op1=ALU.add,
                )
            y_of[chunk, i] = y

        def turn(chunk, i):
            y_words = y_of[chunk, i][:].bitcast(F32)
            turned = turned_banks.tile([P, PASSES, PAIR, P], F32, tag="turned")
            for c in narrow_passes(chunk, i):
                transpose_words(
                    nc,
                    [turned[:, c, u, :] for u in range(PAIR)],
                    y_words[:, c * WORDS_PASS : (c + 1) * WORDS_PASS],
                    identity[:],
                )
            turned_of[chunk, i] = turned

        wide_dims = slice(WIDE_TILE * HEAD_DIM, (WIDE_TILE + 1) * HEAD_DIM)

        def widen_a(chunk, c):
            wide_a = work.tile([P, PAIR, PAIR, GROUP, HEAD_DIM // PAIR], F32)
            for u in range(PAIR):
                first = heads_of(c).start + u * GROUP
                nc.scalar.copy(
                    out=wide_a[:, u],
                    in_=a_of[chunk][:, first : first + GROUP, wide_dims].rearrange(
                        "p g (q e) -> p e g q", e=PAIR
                    ),
                )
            wide_a_of[chunk, c] = wide_a

        def scale_v(chunk, c):
            wide_w = work.tile([P, PAIR, PAIR, GROUP, HEAD_DIM // PAIR], F32)
            for n, head in enumerate(heads_of(c)):
                unit = head * TILES + WIDE_TILE
                nc.scalar.activation(
                    out=wide_w[:, n // GROUP, :, n % GROUP, :],
                    in_=v_of[chunk][:, head // GROUP, wide_dims].rearrange("p (q e) -> p e q", e=PAIR),
                    func=ACT.Copy,
                    scale=factor_of[chunk][:, unit : unit + 1],
                )
            wide_w_of[chunk, c] = wide_w

        def add_and_turn(chunk, c):
            terms = [wide_a_of[chunk, c], wide_w_of[chunk, c]]
            wide_bank = turned_banks.tile([P, PACK, P], F32, tag="turned")
            for t in range(PACK):
                for n, term in enumerate(terms):
                    nc.tensor.matmul(
                        out=wide_bank[:, t, :],
                        lhsT=term[:, t // PAIR, t % PAIR].rearrange("p g q -> p (g q)"),
                        rhs=identity[:],
                        is_transpose=True,
                        start=(n == 0),
                        stop=(n == 1),
                    )
            wide_banks_of[chunk, c] = wide_bank

        def grouped_tile(chunk, i):
            part = part_of(chunk, i)
            if (chunk, part) not in grouped_of:
                n = len(parts_of(chunk)[part])
                grouped = parts.tile([P, PASSES, n, P, PACK], BF16, align_bytes=64)
                grouped_of[chunk, part] = grouped
            return grouped_of[chunk, part], parts_of(chunk)[part].index(i)

        def regroup(chunk, i):
            grouped, j = grouped_tile(chunk, i)
            passes = narrow_passes(chunk, i)
            span = slice(passes[0], passes[-1] + 1)
            nc.scalar.copy(
                out=grouped[:].bitcast(F32)[:, span, j],
                in_=turned_of[chunk, i][:, span].rearrange("p c u t -> p c t u"),
            )

        def regroup_wide(chunk, c):
            grouped, j = grouped_tile(chunk, WIDE_TILE)
            nc.scalar.copy(
                out=grouped[:, c, j], in_=wide_banks_of[chunk, c][:].rearrange("p t n -> p n t")
            )

        def quantise(chunk, part):
            width = len(parts_of(chunk)[part]) * P
            codes = parts.tile([P, PASSES, width], U32, align_bytes=64)
            scales = parts.tile([P, PASSES, width], U8, align_bytes=64)
            nc.vector.quantize_mx(
                out=codes[:].rearrange("p c t -> p (c t)").bitcast(FP8X4),
                scales=scales[:].rearrange("p c t -> p (c t)"),
                in_=grouped_of[chunk, part][:].rearrange("p c j t k -> p (c j t k)"),
            )
            codes_of[chunk, part], scales_of[chunk, part] = codes, scales

        def multiply(chunk, part):
            codes, scales = codes_of[chunk, part], scales_of[chunk, part]
            width = len(parts_of(chunk)[part]) * P
            sums = sum_banks.tile([P, HALVES, width], F32)
            for half in range(HALVES):
                channels = slice(half * P, (half + 1) * P)
                for c in range(PASSES):
                    nc.tensor.matmul_mx(
                        out=sums[:, half, :],
                        lhsT=wo_codes[:, c, channels].bitcast(FP8X4),
                        lhsT_scale=wo_scales[:, c, channels],
                        rhs=codes[:, c, :].bitcast(FP8X4),
                        rhs_scale=scales[:, c, :],
                        start=(c == 0),
                        stop=(c == PASSES - 1),
                    )
            sums_of[chunk, part] = sums

        def apply_gain(chunk, part):
            width = len(parts_of(chunk)[part]) * P
            scaled = parts.tile([P, HALVES, width], F32)
            for half in range(HALVES):
                nc.scalar.activation(
                    out=scaled[:, half, :],
                    in_=sums_of[chunk, part][:, half, :],
                    func=ACT.Copy,
                    scale=gain_column[:, half : half + 1],
                )
            scaled_of[chunk, part] = scaled

        def transpose_back(chunk, part):
            scaled = scaled_of[chunk, part]
            tiles = parts_of(chunk)[part]
            back = out_banks.tile([P, len(tiles), CHANNELS], F32)
            for j, i in enumerate(tiles):
                for half in range(HALVES):
                    nc.tensor.matmul(
                        out=back[:, j, half * P : (half + 1) * P],
                        lhsT=scaled[:, half, j * P : (j + 1) * P],
                        rhs=identity[:],
                        is_transpose=True,
                        start=(half == 0),
                        stop=(half == HALVES - 1 and not adds_on_tensor(chunk)),
                    )
                if adds_on_tensor(chunk):
                    nc.tensor.matmul(
                        out=back[:, j, :],
                        lhsT=identity_bf16[:],
                        rhs=x_of[chunk][:, i * CHANNELS : (i + 1) * CHANNELS],
                        start=False,
                        stop=True,
                    )
            back_of[chunk, part] = back

        def finish(chunk, part):
            b, tokens = tokens_of(chunk)
            tiles = parts_of(chunk)[part]
            span = slice(tiles[0], tiles[-1] + 1)
            result = parts.tile([P, len(tiles), CHANNELS], F32)
            if adds_on_tensor(chunk):
                nc.scalar.copy(out=result[:], in_=back_of[chunk, part][:])
            else:
                nc.vector.tensor_tensor(
                    out=result[:].rearrange("p j n -> p (j n)"),
                    in0=back_of[chunk, part][:].rearrange("p j n -> p (j n)"),
                    in1=x_of[chunk][:, span.start * CHANNELS : span.stop * CHANNELS],
                    op=ALU.add,
                )
            nc.sync.dma_start(
                out=out[b, tokens, :].rearrange("(p i) n -> p i n", i=TILES)[:, span, :],
                in_=result[:],
            )

        def exists(chunk):
            return 0 <= chunk < CHUNKS

        def projected_in(slot):
            chunk, i = divmod(slot - 2 * TILES - 2, TILES)
            return (chunk, i) if exists(chunk) else None

        def part_ending_in(slot):
            here = projected_in(slot)
            if here is None:
                return None
            chunk, i = here
            part = part_of(chunk, i)
            return (chunk, part) if i == parts_of(chunk)[part][-1] else None

        def part_quantised_in(slot):
            for lag in (2, 3):
                ending = part_ending_in(slot - lag)
                if ending is not None and lag == (3 if ending[0] in (5, 6) else 2):
                    return ending
            return None

        for slot in range(TILES * (CHUNKS + 2) + 11):
            n, q = divmod(slot, TILES)
            ahead, dots, now = n, n - 1, n - 2
            here, before = projected_in(slot), projected_in(slot - 1)
            if before is not None and not narrow_passes(*before):
                before = None
            if here is not None and not narrow_passes(*here):
                here = None
            quantised, multiplied = part_quantised_in(slot), part_quantised_in(slot - 1)
            turned_back, finished = part_quantised_in(slot - 2), part_quantised_in(slot - 3)
            if slot == 0:
                for chunk in range(3):
                    load(chunk)
                load_wo_and_gain()
            if q == 0:
                if slot > 0 and exists(ahead + 3 - 1):
                    load(ahead + 3 - 1)
                if exists(now):
                    load_residual(now)
            if q == 0 and exists(now):
                copy_phase_sums(now)
            if q == 0 and exists(now - 1):
                for c in WIDE_PASSES[now - 1]:
                    regroup_wide(now - 1, c)
            if finished is not None and finished[0] < CHUNKS - 1:
                finish(*finished)
            if exists(ahead):
                multiply_elements(ahead, q)
            if before is not None:
                turn(*before)
            if multiplied is not None:
                multiply(*multiplied)
            if q == 0 and exists(now):
                add_phases(now)
            if exists(dots):
                sum_products(dots, q)
            if turned_back is not None:
                transpose_back(*turned_back)
            if q == 2 and exists(now):
                for c in WIDE_PASSES[now]:
                    scale_v(now, c)
            if multiplied is not None:
                apply_gain(*multiplied)
            if before is not None:
                regroup(*before)
            if q == 3 and exists(now):
                for c in WIDE_PASSES[now]:
                    add_and_turn(now, c)
            if exists(ahead):
                squared_norms(ahead, [q])
            if q == 1 and exists(now):
                for c in WIDE_PASSES[now]:
                    widen_a(now, c)
            if q == 0 and exists(now):
                floor_norms(now)
            if here is not None:
                project(*here)
            if q == 0 and exists(now):
                invert_norms(now)
            if q == 1 and exists(now):
                factors(now)
            if quantised is not None:
                quantise(*quantised)
            if finished is not None and finished[0] == CHUNKS - 1:
                finish(*finished)
            if slot == 12:
                turn_wo_and_gain()
            if slot == 13:
                quantise_wo()
